import numpy as np
import ml_dtypes


def mxq(x, axis, fmt="e4m3"):
    dtype, down = {"e4m3": (ml_dtypes.float8_e4m3fn, 7), "e5m2": (ml_dtypes.float8_e5m2, 14)}[fmt]
    v = np.moveaxis(np.asarray(x, np.float32).astype(ml_dtypes.bfloat16).astype(np.float64), axis, -1)
    blocks = v.reshape(v.shape[:-1] + (-1, 32))
    amax = np.abs(blocks).max(-1, keepdims=True)
    byte = np.maximum(np.where(amax > 0, np.frexp(amax)[1] - 1 + 127, 0) - down, 1)
    scale = np.exp2(byte - 127.0)
    codes = (blocks / scale).astype(np.float32).astype(dtype).astype(np.float64)
    return np.moveaxis((codes * scale).reshape(v.shape), -1, axis)


WIDE = False


def mx_kscale(k):
    if not WIDE:
        return np.ones(k)
    levels = np.array([10, -10, 5, -5, 0])
    a = np.random.permutation(np.resize(levels, k // 512 * 4)).reshape(k // 512, 4)
    idx = np.arange(k)
    return np.exp2(a[idx // 512, idx % 128 // 32])


BF16 = ml_dtypes.bfloat16


def bf(x):
    return np.asarray(x, np.float32).astype(BF16)


def f64(x):
    return np.asarray(x).astype(np.float64)


B, DETER, STOCH, ACT, HID, BLOCKS, NIN, NG = 256, 4096, 1024, 512, 512, 8, 3, 3
DPB = DETER // BLOCKS
XW = NIN * HID
EPS = 1e-4


def silu(v):
    return v / (1.0 + np.exp(-v))


def rmsnorm(v, g):
    return v * (1.0 / np.sqrt(np.mean(v * v, axis=-1, keepdims=True) + EPS)) * g


def setup_inputs():
    s, t = mx_kscale(DETER), mx_kscale(STOCH)
    n = np.random.standard_normal
    hw0 = n((BLOCKS, DPB + XW, DPB)) / np.sqrt(DPB + XW)
    hw0[:, :DPB] = hw0[:, :DPB] / s.reshape(BLOCKS, DPB, 1)
    return {"deter": bf(n((B, DETER)) * s), "stoch": bf(n((B, STOCH)) * t), "action": bf(n((B, ACT))),
            "w0": bf(n((DETER, HID)) / np.sqrt(DETER) / s[:, None]), "b0": bf(n(HID) * 0.2), "g0": bf(1.0 + n(HID) * 0.1),
            "w1": bf(n((STOCH, HID)) / np.sqrt(STOCH) / t[:, None]), "b1": bf(n(HID) * 0.2), "g1": bf(1.0 + n(HID) * 0.1),
            "w2": bf(n((ACT, HID)) / np.sqrt(ACT)), "b2": bf(n(HID) * 0.2), "g2": bf(1.0 + n(HID) * 0.1),
            "hw0": bf(hw0), "hb0": bf(n(DETER) * 0.1), "hg0": bf(1.0 + n(DETER) * 0.1)}


def reference(deter, stoch, action, w0, b0, g0, w1, b1, g1, w2, b2, g2, hw0, hb0, hg0):
    dq = mxq(f64(deter), 1, "e4m3")
    a = f64(action)
    a = a / np.maximum(np.abs(a), 1.0)
    x0 = silu(rmsnorm((dq @ mxq(f64(w0), 0, "e4m3")) + f64(b0), f64(g0)))
    x1 = silu(rmsnorm((mxq(f64(stoch), 1, "e4m3") @ mxq(f64(w1), 0, "e4m3")) + f64(b1), f64(g1)))
    x2 = silu(rmsnorm((mxq(a, 1, "e4m3") @ mxq(f64(w2), 0, "e4m3")) + f64(b2), f64(g2)))
    xq = mxq(np.concatenate([x0, x1, x2], axis=-1), 1, "e4m3")
    hq = mxq(f64(hw0), 1, "e4m3")
    dg = dq.reshape(B, BLOCKS, DPB).transpose(1, 0, 2)
    y = (dg @ hq[:, :DPB]) + (xq @ hq[:, DPB:])
    y = y.transpose(1, 0, 2).reshape(B, DETER) + f64(hb0)
    return silu(rmsnorm(y, f64(hg0)))

@@ -1,0 +1,257 @@
+import math
+from contextlib import ExitStack
+
+import concourse.mybir as mybir
+from concourse.masks import make_identity
+
+BF16 = mybir.dt.bfloat16
+F32 = mybir.dt.float32
+I32 = mybir.dt.int32
+U32 = mybir.dt.uint32
+U8 = mybir.dt.uint8
+FP8X4 = mybir.dt.float8_e4m3fn_x4
+ALU = mybir.AluOpType
+FUNC = mybir.ActivationFunctionType
+
+P = 128
+PACK = 4
+K_PASS = P * PACK
+BATCH, DETER, STOCH, ACTION, HID, BLOCKS = 256, 4096, 1024, 512, 512, 8
+M_TILES = BATCH // P
+ROWS = M_TILES * P
+BRANCHES = 3
+EPS = 1e-4
+LOAD_PASSES = 4
+RUN = 4
+VECTOR_COLS = 288
+
+FLOPS = 2 * BATCH * (DETER + STOCH + ACTION) * HID + 2 * BATCH * (DETER // BLOCKS + BRANCHES * HID) * DETER
+
+
+def tile_deter_pa_kernel(
+    tc, deter, stoch, action, w0, b0, g0, w1, b1, g1, w2, b2, g2, hw0, hb0, hg0, out
+):
+    nc = tc.nc
+    with ExitStack() as stack:
+        const = stack.enter_context(tc.tile_pool(name="const", bufs=1))
+        keep = stack.enter_context(tc.tile_pool(name="keep", bufs=1))
+        acts = stack.enter_context(tc.tile_pool(name="acts", bufs=2))
+        raw_pool = stack.enter_context(tc.tile_pool(name="raw", bufs=8))
+        grouped_pool = stack.enter_context(tc.tile_pool(name="grouped", bufs=4))
+        packed_pool = stack.enter_context(tc.tile_pool(name="packed", bufs=16))
+        work = stack.enter_context(tc.tile_pool(name="work", bufs=3))
+        small = stack.enter_context(tc.tile_pool(name="small", bufs=4))
+        acc_pool = stack.enter_context(tc.psum_pool(name="acc", bufs=5))
+        turn_pool = stack.enter_context(tc.psum_pool(name="turn", bufs=3))
+
+        warm = const.tile([P, 1], F32)
+        nc.vector.memset(warm[:], 0.0)
+        nc.scalar.activation(out=warm[:], in_=warm[:], func=FUNC.Silu)
+        ident_f32 = const.tile([P, P], F32)
+        make_identity(nc, ident_f32[:])
+        ident_bf16 = const.tile([P, P], BF16)
+        make_identity(nc, ident_bf16[:])
+        ones = const.tile([P, P], BF16)
+        nc.vector.memset(ones[:], 1.0)
+        minus_half = const.tile([P, 1], F32)
+        nc.vector.memset(minus_half[:], -0.5)
+        vector_row = const.tile([P, DETER], BF16)
+        nc.vector.memset(vector_row[:].bitcast(I32), 0)
+
+        def spread(vectors, dest):
+            width = 0
+            for vec in vectors:
+                n = vec.shape[0]
+                nc.scalar.dma_start(
+                    out=vector_row[0:1, width : width + n], in_=vec.rearrange("(o n) -> o n", o=1)
+                )
+                width += n
+            for c in range(0, width, 2 * HID):
+                bank = turn_pool.tile([P, 2 * HID], BF16, name="bank", tag="turn")
+                for h in (0, HID):
+                    nc.tensor.matmul(
+                        bank[:, h : h + HID],
+                        lhsT=ones[:],
+                        rhs=vector_row[:, c + h : c + h + HID],
+                        start=True,
+                        stop=True,
+                    )
+                nc.scalar.copy(out=dest[:, c : c + 2 * HID], in_=bank[:])
+
+        def quantise_weight_pass(rows):
+            raw = raw_pool.tile([P, PACK, HID], BF16, name="raw")
+            nc.sync.dma_start(out=raw[:], in_=rows.rearrange("(p t) n -> p t n", t=PACK))
+            grouped = grouped_pool.tile([P, HID, PACK], BF16, name="grouped", align_bytes=64)
+            src = raw[:].rearrange("p t (c i) -> p c t i", i=RUN)
+            dst = grouped[:].rearrange("p (c i) t -> p c t i", i=RUN)
+            split = VECTOR_COLS // RUN
+            nc.vector.tensor_copy(out=dst[:, :split], in_=src[:, :split])
+            nc.scalar.copy(out=dst[:, split:], in_=src[:, split:])
+            codes = packed_pool.tile([P, HID], U32, name="codes", align_bytes=64)
+            scales = packed_pool.tile([P, HID], U8, name="scales", align_bytes=64)
+            nc.vector.quantize_mx(
+                out=codes[:].bitcast(FP8X4),
+                scales=scales[:],
+                in_=grouped[:].rearrange("p n t -> p (n t)"),
+            )
+            return codes, scales
+
+        def quantise_rows(grouped, codes, scales):
+            nc.vector.quantize_mx(
+                out=codes.bitcast(FP8X4), scales=scales, in_=grouped[:].rearrange("p r t -> p (r t)")
+            )
+
+        def inverse_rms(mean_sq):
+            rstd = small.tile([P, 1], F32, name="rstd")
+            nc.gpsimd.tensor_scalar(
+                out=rstd[:], in0=mean_sq, scalar1=1.0, scalar2=EPS, op0=ALU.mult, op1=ALU.add
+            )
+            nc.gpsimd.tensor_tensor(out=rstd[:], in0=rstd[:], in1=minus_half[:], op=ALU.pow)
+            return rstd
+
+        deter_codes = keep.tile([P, DETER // K_PASS, ROWS], U32, align_bytes=64)
+        deter_scales = keep.tile([P, DETER // K_PASS, ROWS], U8, align_bytes=64)
+        stoch_codes = keep.tile([P, STOCH // K_PASS, ROWS], U32, align_bytes=64)
+        stoch_scales = keep.tile([P, STOCH // K_PASS, ROWS], U8, align_bytes=64)
+        action_codes = keep.tile([P, ACTION // K_PASS, ROWS], U32, align_bytes=64)
+        action_scales = keep.tile([P, ACTION // K_PASS, ROWS], U8, align_bytes=64)
+        x_codes = keep.tile([P, BRANCHES, ROWS], U32, align_bytes=64)
+        x_scales = keep.tile([P, BRANCHES, ROWS], U8, align_bytes=64)
+
+        branch_vectors = keep.tile([P, 2 * BRANCHES, HID], BF16)
+        hb_all = keep.tile([P, DETER], BF16)
+        hg_all = keep.tile([P, DETER], BF16)
+
+        branches = (
+            (deter, w0, deter_codes, deter_scales, False),
+            (stoch, w1, stoch_codes, stoch_scales, False),
+            (action, w2, action_codes, action_scales, True),
+        )
+        for i, (x_in, w_in, in_codes, in_scales, clamp) in enumerate(branches):
+            passes = x_in.shape[1] // K_PASS
+            acc = [acc_pool.tile([P, HID], F32, name="acc%d" % m, tag="acc") for m in range(M_TILES)]
+            for g in range(passes):
+                w_codes, w_scales = quantise_weight_pass(w_in[g * K_PASS : (g + 1) * K_PASS, :])
+                if g % LOAD_PASSES == 0:
+                    n = min(LOAD_PASSES, passes - g) * K_PASS
+                    x_sb = acts.tile([P, M_TILES, LOAD_PASSES * K_PASS], BF16, name="x_sb")
+                    for m in range(M_TILES):
+                        nc.sync.dma_start(
+                            out=x_sb[:, m, :n], in_=x_in[m * P : (m + 1) * P, g * K_PASS : g * K_PASS + n]
+                        )
+                words = x_sb[:].bitcast(F32)
+                first = (g % LOAD_PASSES) * (K_PASS // 2)
+                turned = turn_pool.tile([P, 2, M_TILES, P], F32, name="turned", tag="turn")
+                for m in range(M_TILES):
+                    for u in range(2):
+                        nc.tensor.transpose(
+                            turned[:, u, m, :], words[:, m, first + u : first + K_PASS // 2 : 2], ident_f32[:]
+                        )
+                grouped = grouped_pool.tile([P, ROWS, PACK], BF16, name="grouped_rows", align_bytes=64)
+                if clamp:
+                    nc.vector.tensor_scalar(
+                        out=grouped[:].rearrange("p r (u e) -> p r u e", e=2),
+                        in0=turned[:].bitcast(BF16).rearrange("p u m (b e) -> p (m b) u e", e=2),
+                        scalar1=-1.0,
+                        scalar2=1.0,
+                        op0=ALU.max,
+                        op1=ALU.min,
+                    )
+                else:
+                    nc.scalar.copy(out=grouped[:].bitcast(F32), in_=turned[:].rearrange("p u m b -> p (m b) u"))
+                quantise_rows(grouped, in_codes[:, g, :], in_scales[:, g, :])
+                for m in range(M_TILES):
+                    nc.tensor.matmul_mx(
+                        out=acc[m][:],
+                        lhsT=in_codes[:, g, m * P : (m + 1) * P].bitcast(FP8X4),
+                        lhsT_scale=in_scales[:, g, m * P : (m + 1) * P],
+                        rhs=w_codes[:].bitcast(FP8X4),
+                        rhs_scale=w_scales[:],
+                        start=(g == 0),
+                        stop=(g == passes - 1),
+                    )
+            if i == 0:
+                spread((b0, g0, b1, g1, b2, g2), branch_vectors[:].rearrange("p v n -> p (v n)"))
+
+            x_turned = turn_pool.tile([P, PACK, M_TILES, P], BF16, name="x_turned", tag="turn")
+            for m in range(M_TILES):
+                u_sb = work.tile([P, HID], F32, name="u_sb")
+                nc.vector.tensor_tensor(out=u_sb[:], in0=acc[m][:], in1=branch_vectors[:, 2 * i, :], op=ALU.add)
+                squares = work.tile([P, HID], BF16, name="squares")
+                mean_sq = small.tile([P, 1], F32, name="mean_sq")
+                nc.scalar.activation(
+                    out=squares[:], in_=u_sb[:], func=FUNC.Square, scale=1.0 / math.sqrt(HID), accum_out=mean_sq[:]
+                )
+                rstd = inverse_rms(mean_sq[:])
+                nc.vector.scalar_tensor_tensor(
+                    out=u_sb[:],
+                    in0=u_sb[:],
+                    scalar=rstd[:],
+                    in1=branch_vectors[:, 2 * i + 1, :],
+                    op0=ALU.mult,
+                    op1=ALU.mult,
+                )
+                x_sorted = work.tile([P, PACK, P], BF16, name="x_sorted")
+                nc.scalar.activation(
+                    out=x_sorted[:].rearrange("b t p -> b p t"),
+                    in_=u_sb[:].rearrange("b (p t) -> b p t", t=PACK),
+                    func=FUNC.Silu,
+                )
+                for t in range(PACK):
+                    nc.tensor.transpose(x_turned[:, t, m, :], x_sorted[:, t, :], ident_bf16[:])
+            grouped = grouped_pool.tile([P, ROWS, PACK], BF16, name="grouped_rows", align_bytes=64)
+            nc.scalar.copy(out=grouped[:], in_=x_turned[:].rearrange("p t m b -> p (m b) t"))
+            quantise_rows(grouped, x_codes[:, i, :], x_scales[:, i, :])
+
+        spread((hb0,), hb_all[:])
+        spread((hg0,), hg_all[:])
+
+        y_sb = [keep.tile([P, DETER], F32, name="y_sb%d" % m) for m in range(M_TILES)]
+        block_mean_sq = [keep.tile([P, BLOCKS], F32, name="block_mean_sq%d" % m) for m in range(M_TILES)]
+        passes = 1 + BRANCHES
+        for j in range(BLOCKS):
+            cols = slice(j * HID, (j + 1) * HID)
+            h_packed = [quantise_weight_pass(hw0[j, c * K_PASS : (c + 1) * K_PASS, :]) for c in range(passes)]
+            for m in range(M_TILES):
+                rows = slice(m * P, (m + 1) * P)
+                y_acc = acc_pool.tile([P, HID], F32, name="y_acc", tag="acc")
+                for c in range(passes):
+                    if c == 0:
+                        lhs_codes, lhs_scales = deter_codes[:, j, rows], deter_scales[:, j, rows]
+                    else:
+                        lhs_codes, lhs_scales = x_codes[:, c - 1, rows], x_scales[:, c - 1, rows]
+                    nc.tensor.matmul_mx(
+                        out=y_acc[:],
+                        lhsT=lhs_codes.bitcast(FP8X4),
+                        lhsT_scale=lhs_scales,
+                        rhs=h_packed[c][0][:].bitcast(FP8X4),
+                        rhs_scale=h_packed[c][1][:],
+                        start=(c == 0),
+                        stop=(c == passes - 1),
+                    )
+                nc.vector.tensor_tensor(out=y_sb[m][:, cols], in0=y_acc[:], in1=hb_all[:, cols], op=ALU.add)
+                squares = work.tile([P, HID], BF16, name="squares")
+                nc.scalar.activation(
+                    out=squares[:],
+                    in_=y_sb[m][:, cols],
+                    func=FUNC.Square,
+                    scale=1.0 / math.sqrt(DETER),
+                    accum_out=block_mean_sq[m][:, j : j + 1],
+                )
+
+        for m in range(M_TILES):
+            mean_sq = small.tile([P, 1], F32, name="mean_sq")
+            nc.vector.reduce_sum(out=mean_sq[:], in_=block_mean_sq[m][:], axis=mybir.AxisListType.X)
+            rstd = inverse_rms(mean_sq[:])
+            for j in range(BLOCKS):
+                cols = slice(j * HID, (j + 1) * HID)
+                nc.vector.scalar_tensor_tensor(
+                    out=y_sb[m][:, cols],
+                    in0=y_sb[m][:, cols],
+                    scalar=rstd[:],
+                    in1=hg_all[:, cols],
+                    op0=ALU.mult,
+                    op1=ALU.mult,
+                )
+                nc.scalar.activation(out=y_sb[m][:, cols], in_=y_sb[m][:, cols], func=FUNC.Silu)
+                nc.sync.dma_start(out=out[m * P : (m + 1) * P, cols], in_=y_sb[m][:, cols])

@@ -16,22 +16,44 @@ FUNC = mybir.ActivationFunctionType
 P = 128
 PACK = 4
 K_PASS = P * PACK
-BATCH, DETER, STOCH, ACTION, HID, BLOCKS = 256, 4096, 1024, 512, 512, 8
+BATCH, DETER, HID, BLOCKS = 256, 4096, 512, 8
 M_TILES = BATCH // P
 ROWS = M_TILES * P
 BRANCHES = 3
+BRANCH_ORDER = (2, 1, 0)
+BLOCK_PASSES = 1 + BRANCHES
 EPS = 1e-4
 LOAD_PASSES = 4
+LOAD_AHEAD = 7
 RUN = 4
-VECTOR_COLS = 288
+STAGE1_VECTOR_COLS = 288
+STAGE2_VECTOR_COLS = 256
 
-FLOPS = 2 * BATCH * (DETER + STOCH + ACTION) * HID + 2 * BATCH * (DETER // BLOCKS + BRANCHES * HID) * DETER
+FLOPS = 2 * BATCH * (DETER + 1024 + 512) * HID + 2 * BATCH * BLOCK_PASSES * K_PASS * DETER
 
 
 def tile_deter_pa_kernel(
     tc, deter, stoch, action, w0, b0, g0, w1, b1, g1, w2, b2, g2, hw0, hb0, hg0, out
 ):
     nc = tc.nc
+    inputs = (deter, stoch, action)
+    weights = (w0, w1, w2)
+
+    weight_rows = []
+    stage1 = []
+    last_pass = {}
+    for i in BRANCH_ORDER:
+        for g in range(inputs[i].shape[1] // K_PASS):
+            weight_rows.append(weights[i][g * K_PASS : (g + 1) * K_PASS, :])
+            stage1.append((i, g))
+        last_pass[i] = len(stage1) - 1
+    block_parts = (0,) + tuple(1 + i for i in BRANCH_ORDER)
+    for j in range(BLOCKS):
+        for part in block_parts:
+            weight_rows.append(hw0[j, part * K_PASS : (part + 1) * K_PASS, :])
+    n_stage1 = len(stage1)
+    n_passes = len(weight_rows)
+
     with ExitStack() as stack:
         const = stack.enter_context(tc.tile_pool(name="const", bufs=1))
         keep = stack.enter_context(tc.tile_pool(name="keep", bufs=1))
@@ -39,197 +61,172 @@ def tile_deter_pa_kernel(
         raw_pool = stack.enter_context(tc.tile_pool(name="raw", bufs=8))
         grouped_pool = stack.enter_context(tc.tile_pool(name="grouped", bufs=4))
         packed_pool = stack.enter_context(tc.tile_pool(name="packed", bufs=16))
-        work = stack.enter_context(tc.tile_pool(name="work", bufs=3))
-        small = stack.enter_context(tc.tile_pool(name="small", bufs=4))
+        work = stack.enter_context(tc.tile_pool(name="work", bufs=4))
+        small = stack.enter_context(tc.tile_pool(name="small", bufs=6))
         acc_pool = stack.enter_context(tc.psum_pool(name="acc", bufs=5))
         turn_pool = stack.enter_context(tc.psum_pool(name="turn", bufs=3))
+        stack.enter_context(tc.manual_schedule())
 
-        warm = const.tile([P, 1], F32)
-        nc.vector.memset(warm[:], 0.0)
-        nc.scalar.activation(out=warm[:], in_=warm[:], func=FUNC.Silu)
-        ident_f32 = const.tile([P, P], F32)
-        make_identity(nc, ident_f32[:])
-        ident_bf16 = const.tile([P, P], BF16)
-        make_identity(nc, ident_bf16[:])
-        ones = const.tile([P, P], BF16)
-        nc.vector.memset(ones[:], 1.0)
-        minus_half = const.tile([P, 1], F32)
-        nc.vector.memset(minus_half[:], -0.5)
-        vector_row = const.tile([P, DETER], BF16)
-        nc.vector.memset(vector_row[:].bitcast(I32), 0)
-
-        def spread(vectors, dest):
-            width = 0
-            for vec in vectors:
-                n = vec.shape[0]
-                nc.scalar.dma_start(
-                    out=vector_row[0:1, width : width + n], in_=vec.rearrange("(o n) -> o n", o=1)
-                )
-                width += n
-            for c in range(0, width, 2 * HID):
-                bank = turn_pool.tile([P, 2 * HID], BF16, name="bank", tag="turn")
-                for h in (0, HID):
-                    nc.tensor.matmul(
-                        bank[:, h : h + HID],
-                        lhsT=ones[:],
-                        rhs=vector_row[:, c + h : c + h + HID],
-                        start=True,
-                        stop=True,
-                    )
-                nc.scalar.copy(out=dest[:, c : c + 2 * HID], in_=bank[:])
-
-        def quantise_weight_pass(rows):
-            raw = raw_pool.tile([P, PACK, HID], BF16, name="raw")
-            nc.sync.dma_start(out=raw[:], in_=rows.rearrange("(p t) n -> p t n", t=PACK))
-            grouped = grouped_pool.tile([P, HID, PACK], BF16, name="grouped", align_bytes=64)
-            src = raw[:].rearrange("p t (c i) -> p c t i", i=RUN)
-            dst = grouped[:].rearrange("p (c i) t -> p c t i", i=RUN)
-            split = VECTOR_COLS // RUN
-            nc.vector.tensor_copy(out=dst[:, :split], in_=src[:, :split])
-            nc.scalar.copy(out=dst[:, split:], in_=src[:, split:])
-            codes = packed_pool.tile([P, HID], U32, name="codes", align_bytes=64)
-            scales = packed_pool.tile([P, HID], U8, name="scales", align_bytes=64)
-            nc.vector.quantize_mx(
-                out=codes[:].bitcast(FP8X4),
-                scales=scales[:],
-                in_=grouped[:].rearrange("p n t -> p (n t)"),
-            )
-            return codes, scales
-
-        def quantise_rows(grouped, codes, scales):
-            nc.vector.quantize_mx(
-                out=codes.bitcast(FP8X4), scales=scales, in_=grouped[:].rearrange("p r t -> p (r t)")
-            )
-
-        def inverse_rms(mean_sq):
-            rstd = small.tile([P, 1], F32, name="rstd")
-            nc.gpsimd.tensor_scalar(
-                out=rstd[:], in0=mean_sq, scalar1=1.0, scalar2=EPS, op0=ALU.mult, op1=ALU.add
-            )
-            nc.gpsimd.tensor_tensor(out=rstd[:], in0=rstd[:], in1=minus_half[:], op=ALU.pow)
-            return rstd
-
-        deter_codes = keep.tile([P, DETER // K_PASS, ROWS], U32, align_bytes=64)
-        deter_scales = keep.tile([P, DETER // K_PASS, ROWS], U8, align_bytes=64)
-        stoch_codes = keep.tile([P, STOCH // K_PASS, ROWS], U32, align_bytes=64)
-        stoch_scales = keep.tile([P, STOCH // K_PASS, ROWS], U8, align_bytes=64)
-        action_codes = keep.tile([P, ACTION // K_PASS, ROWS], U32, align_bytes=64)
-        action_scales = keep.tile([P, ACTION // K_PASS, ROWS], U8, align_bytes=64)
+        in_codes = {}
+        in_scales = {}
+        for i in range(BRANCHES):
+            n = inputs[i].shape[1] // K_PASS
+            in_codes[i] = keep.tile([P, n, ROWS], U32, name="in_codes%d" % i, align_bytes=64)
+            in_scales[i] = keep.tile([P, n, ROWS], U8, name="in_scales%d" % i, align_bytes=64)
         x_codes = keep.tile([P, BRANCHES, ROWS], U32, align_bytes=64)
         x_scales = keep.tile([P, BRANCHES, ROWS], U8, align_bytes=64)
-
         branch_vectors = keep.tile([P, 2 * BRANCHES, HID], BF16)
         hb_all = keep.tile([P, DETER], BF16)
         hg_all = keep.tile([P, DETER], BF16)
-
-        branches = (
-            (deter, w0, deter_codes, deter_scales, False),
-            (stoch, w1, stoch_codes, stoch_scales, False),
-            (action, w2, action_codes, action_scales, True),
-        )
-        for i, (x_in, w_in, in_codes, in_scales, clamp) in enumerate(branches):
-            passes = x_in.shape[1] // K_PASS
-            acc = [acc_pool.tile([P, HID], F32, name="acc%d" % m, tag="acc") for m in range(M_TILES)]
-            for g in range(passes):
-                w_codes, w_scales = quantise_weight_pass(w_in[g * K_PASS : (g + 1) * K_PASS, :])
-                if g % LOAD_PASSES == 0:
-                    n = min(LOAD_PASSES, passes - g) * K_PASS
-                    x_sb = acts.tile([P, M_TILES, LOAD_PASSES * K_PASS], BF16, name="x_sb")
-                    for m in range(M_TILES):
-                        nc.sync.dma_start(
-                            out=x_sb[:, m, :n], in_=x_in[m * P : (m + 1) * P, g * K_PASS : g * K_PASS + n]
-                        )
-                words = x_sb[:].bitcast(F32)
-                first = (g % LOAD_PASSES) * (K_PASS // 2)
-                turned = turn_pool.tile([P, 2, M_TILES, P], F32, name="turned", tag="turn")
-                for m in range(M_TILES):
-                    for u in range(2):
-                        nc.tensor.transpose(
-                            turned[:, u, m, :], words[:, m, first + u : first + K_PASS // 2 : 2], ident_f32[:]
-                        )
-                grouped = grouped_pool.tile([P, ROWS, PACK], BF16, name="grouped_rows", align_bytes=64)
-                if clamp:
-                    nc.vector.tensor_scalar(
-                        out=grouped[:].rearrange("p r (u e) -> p r u e", e=2),
-                        in0=turned[:].bitcast(BF16).rearrange("p u m (b e) -> p (m b) u e", e=2),
-                        scalar1=-1.0,
-                        scalar2=1.0,
-                        op0=ALU.max,
-                        op1=ALU.min,
-                    )
-                else:
-                    nc.scalar.copy(out=grouped[:].bitcast(F32), in_=turned[:].rearrange("p u m b -> p (m b) u"))
-                quantise_rows(grouped, in_codes[:, g, :], in_scales[:, g, :])
-                for m in range(M_TILES):
-                    nc.tensor.matmul_mx(
-                        out=acc[m][:],
-                        lhsT=in_codes[:, g, m * P : (m + 1) * P].bitcast(FP8X4),
-                        lhsT_scale=in_scales[:, g, m * P : (m + 1) * P],
-                        rhs=w_codes[:].bitcast(FP8X4),
-                        rhs_scale=w_scales[:],
-                        start=(g == 0),
-                        stop=(g == passes - 1),
-                    )
-            if i == 0:
-                spread((b0, g0, b1, g1, b2, g2), branch_vectors[:].rearrange("p v n -> p (v n)"))
-
-            x_turned = turn_pool.tile([P, PACK, M_TILES, P], BF16, name="x_turned", tag="turn")
-            for m in range(M_TILES):
-                u_sb = work.tile([P, HID], F32, name="u_sb")
-                nc.vector.tensor_tensor(out=u_sb[:], in0=acc[m][:], in1=branch_vectors[:, 2 * i, :], op=ALU.add)
-                squares = work.tile([P, HID], BF16, name="squares")
-                mean_sq = small.tile([P, 1], F32, name="mean_sq")
-                nc.scalar.activation(
-                    out=squares[:], in_=u_sb[:], func=FUNC.Square, scale=1.0 / math.sqrt(HID), accum_out=mean_sq[:]
-                )
-                rstd = inverse_rms(mean_sq[:])
-                nc.vector.scalar_tensor_tensor(
-                    out=u_sb[:],
-                    in0=u_sb[:],
-                    scalar=rstd[:],
-                    in1=branch_vectors[:, 2 * i + 1, :],
-                    op0=ALU.mult,
-                    op1=ALU.mult,
-                )
-                x_sorted = work.tile([P, PACK, P], BF16, name="x_sorted")
-                nc.scalar.activation(
-                    out=x_sorted[:].rearrange("b t p -> b p t"),
-                    in_=u_sb[:].rearrange("b (p t) -> b p t", t=PACK),
-                    func=FUNC.Silu,
-                )
-                for t in range(PACK):
-                    nc.tensor.transpose(x_turned[:, t, m, :], x_sorted[:, t, :], ident_bf16[:])
-            grouped = grouped_pool.tile([P, ROWS, PACK], BF16, name="grouped_rows", align_bytes=64)
-            nc.scalar.copy(out=grouped[:], in_=x_turned[:].rearrange("p t m b -> p (m b) t"))
-            quantise_rows(grouped, x_codes[:, i, :], x_scales[:, i, :])
-
-        spread((hb0,), hb_all[:])
-        spread((hg0,), hg_all[:])
-
         y_sb = [keep.tile([P, DETER], F32, name="y_sb%d" % m) for m in range(M_TILES)]
         block_mean_sq = [keep.tile([P, BLOCKS], F32, name="block_mean_sq%d" % m) for m in range(M_TILES)]
-        passes = 1 + BRANCHES
-        for j in range(BLOCKS):
-            cols = slice(j * HID, (j + 1) * HID)
-            h_packed = [quantise_weight_pass(hw0[j, c * K_PASS : (c + 1) * K_PASS, :]) for c in range(passes)]
-            for m in range(M_TILES):
-                rows = slice(m * P, (m + 1) * P)
-                y_acc = acc_pool.tile([P, HID], F32, name="y_acc", tag="acc")
-                for c in range(passes):
-                    if c == 0:
-                        lhs_codes, lhs_scales = deter_codes[:, j, rows], deter_scales[:, j, rows]
-                    else:
-                        lhs_codes, lhs_scales = x_codes[:, c - 1, rows], x_scales[:, c - 1, rows]
-                    nc.tensor.matmul_mx(
-                        out=y_acc[:],
-                        lhsT=lhs_codes.bitcast(FP8X4),
-                        lhsT_scale=lhs_scales,
-                        rhs=h_packed[c][0][:].bitcast(FP8X4),
-                        rhs_scale=h_packed[c][1][:],
-                        start=(c == 0),
-                        stop=(c == passes - 1),
+
+        raw = {}
+        grouped = {}
+        packed = {}
+        x_sb = {}
+        turned = {}
+        grouped_rows = {}
+        acc = {}
+        u_sb = {}
+        rstd = {}
+        x_turned = {}
+
+        def load(p):
+            raw[p] = raw_pool.tile([P, PACK, HID], BF16, name="raw")
+            nc.sync.dma_start(out=raw[p][:], in_=weight_rows[p].rearrange("(q t) n -> q t n", t=PACK))
+            if p < n_stage1 and stage1[p][1] % LOAD_PASSES == 0:
+                i, g = stage1[p]
+                n = min(LOAD_PASSES * K_PASS, inputs[i].shape[1] - g * K_PASS)
+                x_sb[p] = acts.tile([P, M_TILES, n], BF16, name="x_sb%d" % i)
+                for m in range(M_TILES):
+                    nc.sync.dma_start(
+                        out=x_sb[p][:, m, :], in_=inputs[i][m * P : (m + 1) * P, g * K_PASS : g * K_PASS + n]
                     )
-                nc.vector.tensor_tensor(out=y_sb[m][:, cols], in0=y_acc[:], in1=hb_all[:, cols], op=ALU.add)
+            if p == n_stage1:
+                nc.sync.dma_start(out=hb_all[:], in_=hb0.partition_broadcast(P))
+            if p == n_passes - 1:
+                nc.sync.dma_start(out=hg_all[:], in_=hg0.partition_broadcast(P))
+
+        def regroup(p):
+            grouped[p] = grouped_pool.tile([P, HID, PACK], BF16, name="grouped", align_bytes=64)
+            src = raw[p][:].rearrange("q t (c i) -> q c t i", i=RUN)
+            dst = grouped[p][:].rearrange("q (c i) t -> q c t i", i=RUN)
+            split = (STAGE1_VECTOR_COLS if p < n_stage1 else STAGE2_VECTOR_COLS) // RUN
+            nc.vector.tensor_copy(out=dst[:, :split], in_=src[:, :split])
+            nc.scalar.copy(out=dst[:, split:], in_=src[:, split:])
+
+        def quantise(p):
+            codes = packed_pool.tile([P, HID], U32, name="codes", align_bytes=64)
+            scales = packed_pool.tile([P, HID], U8, name="scales", align_bytes=64)
+            nc.vector.quantize_mx(
+                out=codes[:].bitcast(FP8X4), scales=scales[:], in_=grouped[p][:].rearrange("q n t -> q (n t)")
+            )
+            packed[p] = (codes, scales)
+
+        def turn(p):
+            g = stage1[p][1]
+            words = x_sb[p - g % LOAD_PASSES][:].bitcast(F32)
+            first = (g % LOAD_PASSES) * (K_PASS // 2)
+            turned[p] = turn_pool.tile([P, 2, M_TILES, P], F32, name="turned", tag="turn")
+            for m in range(M_TILES):
+                for u in range(2):
+                    nc.tensor.transpose(
+                        turned[p][:, u, m, :], words[:, m, first + u : first + K_PASS // 2 : 2], ident_f32[:]
+                    )
+
+        def empty(p):
+            grouped_rows[p] = grouped_pool.tile([P, ROWS, PACK], BF16, name="grouped_rows", align_bytes=64)
+            if stage1[p][0] == 2:
+                nc.vector.tensor_scalar(
+                    out=grouped_rows[p][:].rearrange("q r (u e) -> q r u e", e=2),
+                    in0=turned[p][:].bitcast(BF16).rearrange("q u m (b e) -> q (m b) u e", e=2),
+                    scalar1=-1.0,
+                    scalar2=1.0,
+                    op0=ALU.max,
+                    op1=ALU.min,
+                )
+            else:
+                nc.scalar.copy(
+                    out=grouped_rows[p][:].bitcast(F32), in_=turned[p][:].rearrange("q u m b -> q (m b) u")
+                )
+
+        def quantise_rows(tile, codes, scales):
+            nc.vector.quantize_mx(
+                out=codes.bitcast(FP8X4), scales=scales, in_=tile[:].rearrange("q r t -> q (r t)")
+            )
+
+        def multiply(p, acc_tiles, lhs_codes, lhs_scales, start, stop):
+            for m in range(M_TILES):
+                nc.tensor.matmul_mx(
+                    out=acc_tiles[m][:],
+                    lhsT=lhs_codes[:, m * P : (m + 1) * P].bitcast(FP8X4),
+                    lhsT_scale=lhs_scales[:, m * P : (m + 1) * P],
+                    rhs=packed[p][0][:].bitcast(FP8X4),
+                    rhs_scale=packed[p][1][:],
+                    start=start,
+                    stop=stop,
+                )
+
+        def new_acc():
+            return [acc_pool.tile([P, HID], F32, name="acc%d" % m, tag="acc") for m in range(M_TILES)]
+
+        def inverse_rms(mean_sq):
+            result = small.tile([P, 1], F32, name="rstd")
+            nc.gpsimd.tensor_scalar(
+                out=result[:], in0=mean_sq, scalar1=1.0, scalar2=EPS, op0=ALU.mult, op1=ALU.add
+            )
+            nc.gpsimd.tensor_tensor(out=result[:], in0=result[:], in1=minus_half[:], op=ALU.pow)
+            return result
+
+        def epilogue_step(i, step):
+            if step == 1:
+                for m in range(M_TILES):
+                    u_sb[i, m] = work.tile([P, HID], F32, name="u_sb")
+                    nc.vector.tensor_tensor(
+                        out=u_sb[i, m][:], in0=acc[i][m][:], in1=branch_vectors[:, 2 * i, :], op=ALU.add
+                    )
+                    squares = work.tile([P, HID], BF16, name="squares")
+                    mean_sq = small.tile([P, 1], F32, name="mean_sq")
+                    nc.scalar.activation(
+                        out=squares[:],
+                        in_=u_sb[i, m][:],
+                        func=FUNC.Square,
+                        scale=1.0 / math.sqrt(HID),
+                        accum_out=mean_sq[:],
+                    )
+                    rstd[i, m] = inverse_rms(mean_sq[:])
+            if step == 2:
+                x_turned[i] = turn_pool.tile([P, PACK, M_TILES, P], BF16, name="x_turned", tag="turn")
+                for m in range(M_TILES):
+                    nc.vector.scalar_tensor_tensor(
+                        out=u_sb[i, m][:],
+                        in0=u_sb[i, m][:],
+                        scalar=rstd[i, m][:],
+                        in1=branch_vectors[:, 2 * i + 1, :],
+                        op0=ALU.mult,
+                        op1=ALU.mult,
+                    )
+                    x_sorted = work.tile([P, PACK, P], BF16, name="x_sorted")
+                    nc.scalar.activation(
+                        out=x_sorted[:].rearrange("b t q -> b q t"),
+                        in_=u_sb[i, m][:].rearrange("b (q t) -> b q t", t=PACK),
+                        func=FUNC.Silu,
+                    )
+                    for t in range(PACK):
+                        nc.tensor.transpose(x_turned[i][:, t, m, :], x_sorted[:, t, :], ident_bf16[:])
+            if step == 3:
+                grouped_rows["x", i] = grouped_pool.tile(
+                    [P, ROWS, PACK], BF16, name="grouped_rows", align_bytes=64
+                )
+                nc.scalar.copy(out=grouped_rows["x", i][:], in_=x_turned[i][:].rearrange("q t m b -> q (m b) t"))
+            if step == 4:
+                quantise_rows(grouped_rows["x", i], x_codes[:, i, :], x_scales[:, i, :])
+
+        def finish_block(j):
+            cols = slice(j * HID, (j + 1) * HID)
+            for m in range(M_TILES):
+                nc.vector.tensor_tensor(out=y_sb[m][:, cols], in0=acc["y", j][m][:], in1=hb_all[:, cols], op=ALU.add)
                 squares = work.tile([P, HID], BF16, name="squares")
                 nc.scalar.activation(
                     out=squares[:],
@@ -239,16 +236,78 @@ def tile_deter_pa_kernel(
                     accum_out=block_mean_sq[m][:, j : j + 1],
                 )
 
+        warm = const.tile([P, 1], F32)
+        nc.vector.memset(warm[:], 0.0)
+        nc.scalar.activation(out=warm[:], in_=warm[:], func=FUNC.Silu)
+        vector_row = const.tile([P, 2 * BRANCHES, HID], BF16)
+        nc.vector.memset(vector_row[:].bitcast(I32), 0)
+        for v, vec in enumerate((b0, g0, b1, g1, b2, g2)):
+            nc.scalar.dma_start(out=vector_row[0:1, v, :], in_=vec.rearrange("(o n) -> o n", o=1))
+        for p in range(LOAD_AHEAD):
+            load(p)
+        ones = const.tile([P, P], BF16)
+        nc.vector.memset(ones[:], 1.0)
+        minus_half = const.tile([P, 1], F32)
+        nc.vector.memset(minus_half[:], -0.5)
+        ident_f32 = const.tile([P, P], F32)
+        make_identity(nc, ident_f32[:])
+        ident_bf16 = const.tile([P, P], BF16)
+        make_identity(nc, ident_bf16[:])
+
+        for v in range(0, 2 * BRANCHES, 2):
+            bank = turn_pool.tile([P, 2, HID], BF16, name="bank", tag="turn")
+            for h in range(2):
+                nc.tensor.matmul(bank[:, h, :], lhsT=ones[:], rhs=vector_row[:, v + h, :], start=True, stop=True)
+            nc.scalar.copy(out=branch_vectors[:, v : v + 2, :], in_=bank[:])
+
+        regroup(0)
+        turn(0)
+        turn(1)
+        empty(0)
+        for p in range(n_passes):
+            if p + LOAD_AHEAD < n_passes:
+                load(p + LOAD_AHEAD)
+            if p + 1 < n_passes:
+                regroup(p + 1)
+            if p + 2 < n_stage1:
+                turn(p + 2)
+            if p + 1 < n_stage1:
+                empty(p + 1)
+            quantise(p)
+            if p < n_stage1:
+                i, g = stage1[p]
+                quantise_rows(grouped_rows[p], in_codes[i][:, g, :], in_scales[i][:, g, :])
+            for i in BRANCH_ORDER:
+                if 1 <= p - last_pass[i] <= 4:
+                    epilogue_step(i, p - last_pass[i])
+            if p < n_stage1:
+                i, g = stage1[p]
+                if g == 0:
+                    acc[i] = new_acc()
+                multiply(p, acc[i], in_codes[i][:, g, :], in_scales[i][:, g, :], g == 0, p == last_pass[i])
+            else:
+                j, c = divmod(p - n_stage1, BLOCK_PASSES)
+                if c == 0:
+                    acc["y", j] = new_acc()
+                    multiply(p, acc["y", j], in_codes[0][:, j, :], in_scales[0][:, j, :], True, False)
+                    if j > 0:
+                        finish_block(j - 1)
+                else:
+                    i = block_parts[c] - 1
+                    multiply(p, acc["y", j], x_codes[:, i, :], x_scales[:, i, :], False, c == BLOCK_PASSES - 1)
+        finish_block(BLOCKS - 1)
+
         for m in range(M_TILES):
             mean_sq = small.tile([P, 1], F32, name="mean_sq")
             nc.vector.reduce_sum(out=mean_sq[:], in_=block_mean_sq[m][:], axis=mybir.AxisListType.X)
-            rstd = inverse_rms(mean_sq[:])
+            rstd["y", m] = inverse_rms(mean_sq[:])
+        for m in range(M_TILES):
             for j in range(BLOCKS):
                 cols = slice(j * HID, (j + 1) * HID)
                 nc.vector.scalar_tensor_tensor(
                     out=y_sb[m][:, cols],
                     in0=y_sb[m][:, cols],
-                    scalar=rstd[:],
+                    scalar=rstd["y", m][:],
                     in1=hg_all[:, cols],
                     op0=ALU.mult,
                     op1=ALU.mult,

@@ -25,6 +25,10 @@ BLOCK_PASSES = 1 + BRANCHES
 EPS = 1e-4
 LOAD_PASSES = 4
 LOAD_AHEAD = 7
+MULTIPLY_LAG = 2
+BIAS_LAG = 3
+SQUARE_LAG = 4
+EPILOGUE_STEPS = 6
 RUN = 4
 STAGE1_VECTOR_COLS = 288
 STAGE2_VECTOR_COLS = 256
@@ -180,12 +184,13 @@ def tile_deter_pa_kernel(
             return result
 
         def epilogue_step(i, step):
-            if step == 1:
-                for m in range(M_TILES):
+            for m in range(M_TILES):
+                if step == 1:
                     u_sb[i, m] = work.tile([P, HID], F32, name="u_sb")
                     nc.vector.tensor_tensor(
                         out=u_sb[i, m][:], in0=acc[i][m][:], in1=branch_vectors[:, 2 * i, :], op=ALU.add
                     )
+                if step == 2:
                     squares = work.tile([P, HID], BF16, name="squares")
                     mean_sq = small.tile([P, 1], F32, name="mean_sq")
                     nc.scalar.activation(
@@ -196,9 +201,7 @@ def tile_deter_pa_kernel(
                         accum_out=mean_sq[:],
                     )
                     rstd[i, m] = inverse_rms(mean_sq[:])
-            if step == 2:
-                x_turned[i] = turn_pool.tile([P, PACK, M_TILES, P], BF16, name="x_turned", tag="turn")
-                for m in range(M_TILES):
+                if step == 3:
                     nc.vector.scalar_tensor_tensor(
                         out=u_sb[i, m][:],
                         in0=u_sb[i, m][:],
@@ -207,6 +210,9 @@ def tile_deter_pa_kernel(
                         op0=ALU.mult,
                         op1=ALU.mult,
                     )
+                if step == 4:
+                    if m == 0:
+                        x_turned[i] = turn_pool.tile([P, PACK, M_TILES, P], BF16, name="x_turned", tag="turn")
                     x_sorted = work.tile([P, PACK, P], BF16, name="x_sorted")
                     nc.scalar.activation(
                         out=x_sorted[:].rearrange("b t q -> b q t"),
@@ -215,18 +221,35 @@ def tile_deter_pa_kernel(
                     )
                     for t in range(PACK):
                         nc.tensor.transpose(x_turned[i][:, t, m, :], x_sorted[:, t, :], ident_bf16[:])
-            if step == 3:
+            if step == 5:
                 grouped_rows["x", i] = grouped_pool.tile(
                     [P, ROWS, PACK], BF16, name="grouped_rows", align_bytes=64
                 )
                 nc.scalar.copy(out=grouped_rows["x", i][:], in_=x_turned[i][:].rearrange("q t m b -> q (m b) t"))
-            if step == 4:
+            if step == 6:
                 quantise_rows(grouped_rows["x", i], x_codes[:, i, :], x_scales[:, i, :])
 
-        def finish_block(j):
+        def multiply_block(p):
+            j, c = divmod(p - n_stage1, BLOCK_PASSES)
+            if c == 0:
+                acc["y", j] = new_acc()
+                multiply(p, acc["y", j], in_codes[0][:, j, :], in_scales[0][:, j, :], True, False)
+            else:
+                i = block_parts[c] - 1
+                multiply(p, acc["y", j], x_codes[:, i, :], x_scales[:, i, :], False, c == BLOCK_PASSES - 1)
+
+        def block_that_ends_at(p):
+            j, c = divmod(p - n_stage1, BLOCK_PASSES)
+            return j if (0 <= j < BLOCKS and c == BLOCK_PASSES - 1) else None
+
+        def add_bias(j):
             cols = slice(j * HID, (j + 1) * HID)
             for m in range(M_TILES):
                 nc.vector.tensor_tensor(out=y_sb[m][:, cols], in0=acc["y", j][m][:], in1=hb_all[:, cols], op=ALU.add)
+
+        def mean_of_squares(j):
+            cols = slice(j * HID, (j + 1) * HID)
+            for m in range(M_TILES):
                 squares = work.tile([P, HID], BF16, name="squares")
                 nc.scalar.activation(
                     out=squares[:],
@@ -264,7 +287,7 @@ def tile_deter_pa_kernel(
         turn(0)
         turn(1)
         empty(0)
-        for p in range(n_passes):
+        for p in range(n_passes + SQUARE_LAG + 1):
             if p + LOAD_AHEAD < n_passes:
                 load(p + LOAD_AHEAD)
             if p + 1 < n_passes:
@@ -273,29 +296,23 @@ def tile_deter_pa_kernel(
                 turn(p + 2)
             if p + 1 < n_stage1:
                 empty(p + 1)
-            quantise(p)
+            if p < n_passes:
+                quantise(p)
             if p < n_stage1:
                 i, g = stage1[p]
                 quantise_rows(grouped_rows[p], in_codes[i][:, g, :], in_scales[i][:, g, :])
-            for i in BRANCH_ORDER:
-                if 1 <= p - last_pass[i] <= 4:
-                    epilogue_step(i, p - last_pass[i])
-            if p < n_stage1:
-                i, g = stage1[p]
                 if g == 0:
                     acc[i] = new_acc()
                 multiply(p, acc[i], in_codes[i][:, g, :], in_scales[i][:, g, :], g == 0, p == last_pass[i])
-            else:
-                j, c = divmod(p - n_stage1, BLOCK_PASSES)
-                if c == 0:
-                    acc["y", j] = new_acc()
-                    multiply(p, acc["y", j], in_codes[0][:, j, :], in_scales[0][:, j, :], True, False)
-                    if j > 0:
-                        finish_block(j - 1)
-                else:
-                    i = block_parts[c] - 1
-                    multiply(p, acc["y", j], x_codes[:, i, :], x_scales[:, i, :], False, c == BLOCK_PASSES - 1)
-        finish_block(BLOCKS - 1)
+            for i in BRANCH_ORDER:
+                if 1 <= p - last_pass[i] <= EPILOGUE_STEPS:
+                    epilogue_step(i, p - last_pass[i])
+            if n_stage1 <= p - MULTIPLY_LAG < n_passes:
+                multiply_block(p - MULTIPLY_LAG)
+            if block_that_ends_at(p - BIAS_LAG) is not None:
+                add_bias(block_that_ends_at(p - BIAS_LAG))
+            if block_that_ends_at(p - SQUARE_LAG) is not None:
+                mean_of_squares(block_that_ends_at(p - SQUARE_LAG))
 
         for m in range(M_TILES):
             mean_sq = small.tile([P, 1], F32, name="mean_sq")

@@ -83,7 +83,7 @@ def tile_deter_pa_kernel(
         hb_all = keep.tile([P, DETER], BF16)
         hg_all = keep.tile([P, DETER], BF16)
         y_sb = [keep.tile([P, DETER], F32, name="y_sb%d" % m) for m in range(M_TILES)]
-        block_mean_sq = [keep.tile([P, BLOCKS], F32, name="block_mean_sq%d" % m) for m in range(M_TILES)]
+        block_mean_sq = [keep.tile([P, BLOCKS + 1], F32, name="block_mean_sq%d" % m) for m in range(M_TILES)]
 
         raw = {}
         grouped = {}
@@ -94,6 +94,7 @@ def tile_deter_pa_kernel(
         acc = {}
         u_sb = {}
         rstd = {}
+        mean_sq = {}
         x_turned = {}
 
         def load(p):
@@ -175,12 +176,9 @@ def tile_deter_pa_kernel(
         def new_acc():
             return [acc_pool.tile([P, HID], F32, name="acc%d" % m, tag="acc") for m in range(M_TILES)]
 
-        def inverse_rms(mean_sq):
-            result = small.tile([P, 1], F32, name="rstd")
-            nc.gpsimd.tensor_scalar(
-                out=result[:], in0=mean_sq, scalar1=1.0, scalar2=EPS, op0=ALU.mult, op1=ALU.add
-            )
-            nc.gpsimd.tensor_tensor(out=result[:], in0=result[:], in1=minus_half[:], op=ALU.pow)
+        def power_minus_half(value):
+            result = small.tile(list(value.shape), F32, name="rstd")
+            nc.gpsimd.tensor_tensor(out=result[:], in0=value, in1=minus_half[:, : value.shape[1]], op=ALU.pow)
             return result
 
         def epilogue_step(i, step):
@@ -191,21 +189,21 @@ def tile_deter_pa_kernel(
                         out=u_sb[i, m][:], in0=acc[i][m][:], in1=branch_vectors[:, 2 * i, :], op=ALU.add
                     )
                 if step == 2:
+                    if m == 0:
+                        mean_sq[i] = small.tile([P, M_TILES], F32, name="mean_sq")
                     squares = work.tile([P, HID], BF16, name="squares")
-                    mean_sq = small.tile([P, 1], F32, name="mean_sq")
                     nc.scalar.activation(
                         out=squares[:],
                         in_=u_sb[i, m][:],
                         func=FUNC.Square,
                         scale=1.0 / math.sqrt(HID),
-                        accum_out=mean_sq[:],
+                        accum_out=mean_sq[i][:, m : m + 1],
                     )
-                    rstd[i, m] = inverse_rms(mean_sq[:])
                 if step == 3:
                     nc.vector.scalar_tensor_tensor(
                         out=u_sb[i, m][:],
                         in0=u_sb[i, m][:],
-                        scalar=rstd[i, m][:],
+                        scalar=rstd[i][:, m : m + 1],
                         in1=branch_vectors[:, 2 * i + 1, :],
                         op0=ALU.mult,
                         op1=ALU.mult,
@@ -221,6 +219,9 @@ def tile_deter_pa_kernel(
                     )
                     for t in range(PACK):
                         nc.tensor.transpose(x_turned[i][:, t, m, :], x_sorted[:, t, :], ident_bf16[:])
+            if step == 2:
+                nc.scalar.activation(out=mean_sq[i][:], in_=mean_sq[i][:], func=FUNC.Copy, bias=EPS)
+                rstd[i] = power_minus_half(mean_sq[i][:])
             if step == 5:
                 grouped_rows["x", i] = grouped_pool.tile(
                     [P, ROWS, PACK], BF16, name="grouped_rows", align_bytes=64
@@ -270,8 +271,10 @@ def tile_deter_pa_kernel(
             load(p)
         ones = const.tile([P, P], BF16)
         nc.vector.memset(ones[:], 1.0)
-        minus_half = const.tile([P, 1], F32)
+        minus_half = const.tile([P, M_TILES], F32)
         nc.vector.memset(minus_half[:], -0.5)
+        for m in range(M_TILES):
+            nc.vector.memset(block_mean_sq[m][:], EPS)
         ident_f32 = const.tile([P, P], F32)
         make_identity(nc, ident_f32[:])
         ident_bf16 = const.tile([P, P], BF16)
@@ -315,9 +318,9 @@ def tile_deter_pa_kernel(
                 mean_of_squares(block_that_ends_at(p - SQUARE_LAG))
 
         for m in range(M_TILES):
-            mean_sq = small.tile([P, 1], F32, name="mean_sq")
-            nc.vector.reduce_sum(out=mean_sq[:], in_=block_mean_sq[m][:], axis=mybir.AxisListType.X)
-            rstd["y", m] = inverse_rms(mean_sq[:])
+            mean_sq["y", m] = small.tile([P, 1], F32, name="mean_sq_y")
+            nc.vector.reduce_sum(out=mean_sq["y", m][:], in_=block_mean_sq[m][:], axis=mybir.AxisListType.X)
+            rstd["y", m] = power_minus_half(mean_sq["y", m][:])
         for m in range(M_TILES):
             for j in range(BLOCKS):
                 cols = slice(j * HID, (j + 1) * HID)

@@ -25,12 +25,12 @@ BLOCK_PASSES = 1 + BRANCHES
 EPS = 1e-4
 LOAD_PASSES = 4
 LOAD_AHEAD = 7
-MULTIPLY_LAG = 2
-BIAS_LAG = 3
-SQUARE_LAG = 4
-EPILOGUE_STEPS = 6
+MULTIPLY_LAG = 3
+BIAS_LAG = 4
+SQUARE_LAG = 5
+EPILOGUE_STEPS = 7
 RUN = 4
-STAGE1_VECTOR_COLS = 288
+STAGE1_VECTOR_COLS = 352
 STAGE2_VECTOR_COLS = 256
 
 FLOPS = 2 * BATCH * (DETER + 1024 + 512) * HID + 2 * BATCH * BLOCK_PASSES * K_PASS * DETER
@@ -199,7 +199,7 @@ def tile_deter_pa_kernel(
                         scale=1.0 / math.sqrt(HID),
                         accum_out=mean_sq[i][:, m : m + 1],
                     )
-                if step == 3:
+                if step == 4:
                     nc.vector.scalar_tensor_tensor(
                         out=u_sb[i, m][:],
                         in0=u_sb[i, m][:],
@@ -208,7 +208,7 @@ def tile_deter_pa_kernel(
                         op0=ALU.mult,
                         op1=ALU.mult,
                     )
-                if step == 4:
+                if step == 5:
                     if m == 0:
                         x_turned[i] = turn_pool.tile([P, PACK, M_TILES, P], BF16, name="x_turned", tag="turn")
                     x_sorted = work.tile([P, PACK, P], BF16, name="x_sorted")
@@ -222,12 +222,12 @@ def tile_deter_pa_kernel(
             if step == 2:
                 nc.scalar.activation(out=mean_sq[i][:], in_=mean_sq[i][:], func=FUNC.Copy, bias=EPS)
                 rstd[i] = power_minus_half(mean_sq[i][:])
-            if step == 5:
+            if step == 6:
                 grouped_rows["x", i] = grouped_pool.tile(
                     [P, ROWS, PACK], BF16, name="grouped_rows", align_bytes=64
                 )
                 nc.scalar.copy(out=grouped_rows["x", i][:], in_=x_turned[i][:].rearrange("q t m b -> q (m b) t"))
-            if step == 6:
+            if step == 7:
                 quantise_rows(grouped_rows["x", i], x_codes[:, i, :], x_scales[:, i, :])
 
         def multiply_block(p):

@@ -23,15 +23,16 @@ BRANCHES = 3
 BRANCH_ORDER = (2, 1, 0)
 BLOCK_PASSES = 1 + BRANCHES
 EPS = 1e-4
-LOAD_PASSES = 4
-LOAD_AHEAD = 7
-MULTIPLY_LAG = 3
-BIAS_LAG = 4
-SQUARE_LAG = 5
+LOAD_PASSES = 2
+LOAD_AHEAD = 8
+GROUP_AHEAD = 2
+N_TILES = HID // P
+BLOCK_TURNS = 4
+TURNED_AHEAD = 4
 EPILOGUE_STEPS = 7
 RUN = 4
 STAGE1_VECTOR_COLS = 352
-STAGE2_VECTOR_COLS = 256
+STAGE2_VECTOR_COLS = 288
 
 FLOPS = 2 * BATCH * (DETER + 1024 + 512) * HID + 2 * BATCH * BLOCK_PASSES * K_PASS * DETER
 
@@ -63,12 +64,12 @@ def tile_deter_pa_kernel(
         keep = stack.enter_context(tc.tile_pool(name="keep", bufs=1))
         acts = stack.enter_context(tc.tile_pool(name="acts", bufs=2))
         raw_pool = stack.enter_context(tc.tile_pool(name="raw", bufs=8))
-        grouped_pool = stack.enter_context(tc.tile_pool(name="grouped", bufs=4))
+        grouped_pool = stack.enter_context(tc.tile_pool(name="grouped", bufs=5))
         packed_pool = stack.enter_context(tc.tile_pool(name="packed", bufs=16))
         work = stack.enter_context(tc.tile_pool(name="work", bufs=4))
         small = stack.enter_context(tc.tile_pool(name="small", bufs=6))
-        acc_pool = stack.enter_context(tc.psum_pool(name="acc", bufs=5))
-        turn_pool = stack.enter_context(tc.psum_pool(name="turn", bufs=3))
+        outs = stack.enter_context(tc.tile_pool(name="outs", bufs=8))
+        banks = stack.enter_context(tc.psum_pool(name="banks", bufs=8))
         stack.enter_context(tc.manual_schedule())
 
         in_codes = {}
@@ -80,10 +81,12 @@ def tile_deter_pa_kernel(
         x_codes = keep.tile([P, BRANCHES, ROWS], U32, align_bytes=64)
         x_scales = keep.tile([P, BRANCHES, ROWS], U8, align_bytes=64)
         branch_vectors = keep.tile([P, 2 * BRANCHES, HID], BF16)
-        hb_all = keep.tile([P, DETER], BF16)
+        hb_columns = keep.tile([P, BLOCKS * N_TILES], F32)
         hg_all = keep.tile([P, DETER], BF16)
-        y_sb = [keep.tile([P, DETER], F32, name="y_sb%d" % m) for m in range(M_TILES)]
-        block_mean_sq = [keep.tile([P, BLOCKS + 1], F32, name="block_mean_sq%d" % m) for m in range(M_TILES)]
+        y_sb = keep.tile([P, BLOCKS * N_TILES, ROWS], F32)
+        gram = []
+        y_acc = {}
+        turned_out = {}
 
         raw = {}
         grouped = {}
@@ -108,8 +111,8 @@ def tile_deter_pa_kernel(
                     nc.sync.dma_start(
                         out=x_sb[p][:, m, :], in_=inputs[i][m * P : (m + 1) * P, g * K_PASS : g * K_PASS + n]
                     )
-            if p == n_stage1:
-                nc.sync.dma_start(out=hb_all[:], in_=hb0.partition_broadcast(P))
+            if p == LOAD_AHEAD:
+                nc.sync.dma_start(out=hb_rows[: BLOCKS * N_TILES, :], in_=hb0.rearrange("(c n) -> c n", n=P))
             if p == n_passes - 1:
                 nc.sync.dma_start(out=hg_all[:], in_=hg0.partition_broadcast(P))
 
@@ -133,7 +136,7 @@ def tile_deter_pa_kernel(
             g = stage1[p][1]
             words = x_sb[p - g % LOAD_PASSES][:].bitcast(F32)
             first = (g % LOAD_PASSES) * (K_PASS // 2)
-            turned[p] = turn_pool.tile([P, 2, M_TILES, P], F32, name="turned", tag="turn")
+            turned[p] = banks.tile([P, 2, M_TILES, P], F32, name="turned", tag="bank")
             for m in range(M_TILES):
                 for u in range(2):
                     nc.tensor.transpose(
@@ -174,7 +177,7 @@ def tile_deter_pa_kernel(
                 )
 
         def new_acc():
-            return [acc_pool.tile([P, HID], F32, name="acc%d" % m, tag="acc") for m in range(M_TILES)]
+            return [banks.tile([P, HID], F32, name="acc%d" % m, tag="bank") for m in range(M_TILES)]
 
         def power_minus_half(value):
             result = small.tile(list(value.shape), F32, name="rstd")
@@ -210,7 +213,7 @@ def tile_deter_pa_kernel(
                     )
                 if step == 5:
                     if m == 0:
-                        x_turned[i] = turn_pool.tile([P, PACK, M_TILES, P], BF16, name="x_turned", tag="turn")
+                        x_turned[i] = banks.tile([P, PACK, M_TILES, P], BF16, name="x_turned", tag="bank")
                     x_sorted = work.tile([P, PACK, P], BF16, name="x_sorted")
                     nc.scalar.activation(
                         out=x_sorted[:].rearrange("b t q -> b q t"),
@@ -230,34 +233,68 @@ def tile_deter_pa_kernel(
             if step == 7:
                 quantise_rows(grouped_rows["x", i], x_codes[:, i, :], x_scales[:, i, :])
 
-        def multiply_block(p):
-            j, c = divmod(p - n_stage1, BLOCK_PASSES)
+        def block_operands(j, c):
+            p = n_stage1 + j * BLOCK_PASSES + c
             if c == 0:
-                acc["y", j] = new_acc()
-                multiply(p, acc["y", j], in_codes[0][:, j, :], in_scales[0][:, j, :], True, False)
-            else:
-                i = block_parts[c] - 1
-                multiply(p, acc["y", j], x_codes[:, i, :], x_scales[:, i, :], False, c == BLOCK_PASSES - 1)
+                return packed[p], in_codes[0][:, j, :], in_scales[0][:, j, :]
+            i = block_parts[c] - 1
+            return packed[p], x_codes[:, i, :], x_scales[:, i, :]
 
-        def block_that_ends_at(p):
-            j, c = divmod(p - n_stage1, BLOCK_PASSES)
-            return j if (0 <= j < BLOCKS and c == BLOCK_PASSES - 1) else None
+        def multiply_y(out, j, c, t):
+            (codes, scales), rhs_codes, rhs_scales = block_operands(j, c)
+            cols = slice(t * P, (t + 1) * P)
+            nc.tensor.matmul_mx(
+                out=out,
+                lhsT=codes[:, cols].bitcast(FP8X4),
+                lhsT_scale=scales[:, cols],
+                rhs=rhs_codes.bitcast(FP8X4),
+                rhs_scale=rhs_scales,
+                start=c == 0,
+                stop=c == BLOCK_PASSES - 1,
+            )
 
-        def add_bias(j):
-            cols = slice(j * HID, (j + 1) * HID)
-            for m in range(M_TILES):
-                nc.vector.tensor_tensor(out=y_sb[m][:, cols], in0=acc["y", j][m][:], in1=hb_all[:, cols], op=ALU.add)
+        def multiply_half(j, h):
+            bank = banks.tile([P, 2, ROWS], F32, name="y_acc", tag="bank")
+            for s in range(2):
+                for c in range(BLOCK_PASSES):
+                    multiply_y(bank[:, s, :], j, c, 2 * h + s)
+                y_acc[j, 2 * h + s] = bank[:, s, :]
 
-        def mean_of_squares(j):
-            cols = slice(j * HID, (j + 1) * HID)
-            for m in range(M_TILES):
-                squares = work.tile([P, HID], BF16, name="squares")
+        def add_bias(j, t, engine):
+            n = j * N_TILES + t
+            if engine == "scalar":
                 nc.scalar.activation(
-                    out=squares[:],
-                    in_=y_sb[m][:, cols],
-                    func=FUNC.Square,
-                    scale=1.0 / math.sqrt(DETER),
-                    accum_out=block_mean_sq[m][:, j : j + 1],
+                    out=y_sb[:, n, :], in_=y_acc[j, t], func=FUNC.Identity, bias=hb_columns[:, n : n + 1]
+                )
+            else:
+                nc.vector.tensor_scalar(
+                    out=y_sb[:, n, :], in0=y_acc[j, t], scalar1=hb_columns[:, n : n + 1], scalar2=None, op0=ALU.add
+                )
+
+        def add_to_gram(j, t, m):
+            if j == 0 and t == 0 and m == 0:
+                gram.extend(banks.tile([P, P], F32, name="gram%d" % k, tag="bank") for k in range(M_TILES))
+            y_tile = y_sb[:, j * N_TILES + t, m * P : (m + 1) * P]
+            nc.tensor.matmul(
+                gram[m][:], lhsT=y_tile, rhs=y_tile, start=j == 0 and t == 0, stop=j == BLOCKS - 1 and t == N_TILES - 1
+            )
+
+        def block_step(j, step):
+            if step < 2:
+                multiply_half(j, step)
+            if 1 <= step < 3:
+                for s in range(2):
+                    add_bias(j, 2 * (step - 1) + s, "scalar")
+            if step >= 2:
+                for s in range(2):
+                    for m in range(M_TILES):
+                        add_to_gram(j, 2 * (step - 2) + s, m)
+
+        def turn_out(m, j):
+            turned_out[m, j] = banks.tile([P, N_TILES, P], F32, name="turned_out", tag="bank")
+            for t in range(N_TILES):
+                nc.tensor.transpose(
+                    turned_out[m, j][:, t, :], y_sb[:, j * N_TILES + t, m * P : (m + 1) * P], ident_f32[:]
                 )
 
         warm = const.tile([P, 1], F32)
@@ -265,72 +302,125 @@ def tile_deter_pa_kernel(
         nc.scalar.activation(out=warm[:], in_=warm[:], func=FUNC.Silu)
         vector_row = const.tile([P, 2 * BRANCHES, HID], BF16)
         nc.vector.memset(vector_row[:].bitcast(I32), 0)
-        for v, vec in enumerate((b0, g0, b1, g1, b2, g2)):
-            nc.scalar.dma_start(out=vector_row[0:1, v, :], in_=vec.rearrange("(o n) -> o n", o=1))
+        branch_rows = ((b0, g0), (b1, g1), (b2, g2))
         for p in range(LOAD_AHEAD):
             load(p)
+            if p < BRANCHES:
+                i = BRANCH_ORDER[p]
+                for h, vec in enumerate(branch_rows[i]):
+                    nc.sync.dma_start(out=vector_row[0:1, 2 * i + h, :], in_=vec.rearrange("(o n) -> o n", o=1))
         ones = const.tile([P, P], BF16)
         nc.vector.memset(ones[:], 1.0)
         minus_half = const.tile([P, M_TILES], F32)
         nc.vector.memset(minus_half[:], -0.5)
-        for m in range(M_TILES):
-            nc.vector.memset(block_mean_sq[m][:], EPS)
+        hb_rows = const.tile([P, P], BF16)
+        nc.vector.memset(hb_rows[:].bitcast(I32), 0)
         ident_f32 = const.tile([P, P], F32)
         make_identity(nc, ident_f32[:])
         ident_bf16 = const.tile([P, P], BF16)
         make_identity(nc, ident_bf16[:])
+        ident_mean = const.tile([P, P], F32)
+        nc.scalar.mul(ident_mean[:], ident_f32[:], 1.0 / DETER)
 
-        for v in range(0, 2 * BRANCHES, 2):
-            bank = turn_pool.tile([P, 2, HID], BF16, name="bank", tag="turn")
+        spread = {}
+
+        def spread_vectors(i):
+            spread[i] = banks.tile([P, 2, HID], BF16, name="spread", tag="bank")
             for h in range(2):
-                nc.tensor.matmul(bank[:, h, :], lhsT=ones[:], rhs=vector_row[:, v + h, :], start=True, stop=True)
-            nc.scalar.copy(out=branch_vectors[:, v : v + 2, :], in_=bank[:])
+                nc.tensor.matmul(
+                    spread[i][:, h, :], lhsT=ones[:], rhs=vector_row[:, 2 * i + h, :], start=True, stop=True
+                )
 
-        regroup(0)
+        def empty_spread(i):
+            nc.scalar.copy(out=branch_vectors[:, 2 * i : 2 * i + 2, :], in_=spread[i][:])
+
+        def turn_hb():
+            bank = banks.tile([P, P], BF16, name="hb_bank", tag="bank")
+            nc.tensor.transpose(bank[:], hb_rows[:], ident_bf16[:])
+            nc.scalar.copy(out=hb_columns[:], in_=bank[:, : BLOCKS * N_TILES])
+
+        x_ready = last_pass[0] + EPILOGUE_STEPS
+        last_block = BLOCKS - 1
+        first_turn = [max(n_stage1 + (j + 1) * BLOCK_PASSES, x_ready + 1 + 2 * j) for j in range(last_block)]
+        def group(p):
+            if p < n_passes:
+                regroup(p)
+            if p + 1 < n_stage1:
+                turn(p + 1)
+            if p < n_stage1:
+                empty(p)
+
         turn(0)
-        turn(1)
-        empty(0)
-        for p in range(n_passes + SQUARE_LAG + 1):
+        spread_vectors(BRANCH_ORDER[0])
+        for p in range(GROUP_AHEAD):
+            group(p)
+        for p in range(n_passes):
             if p + LOAD_AHEAD < n_passes:
                 load(p + LOAD_AHEAD)
-            if p + 1 < n_passes:
-                regroup(p + 1)
-            if p + 2 < n_stage1:
-                turn(p + 2)
-            if p + 1 < n_stage1:
-                empty(p + 1)
-            if p < n_passes:
-                quantise(p)
+            quantise(p)
             if p < n_stage1:
                 i, g = stage1[p]
                 quantise_rows(grouped_rows[p], in_codes[i][:, g, :], in_scales[i][:, g, :])
                 if g == 0:
                     acc[i] = new_acc()
                 multiply(p, acc[i], in_codes[i][:, g, :], in_scales[i][:, g, :], g == 0, p == last_pass[i])
+            if p < BRANCHES:
+                empty_spread(BRANCH_ORDER[p])
+            if p + 1 < BRANCHES:
+                spread_vectors(BRANCH_ORDER[p + 1])
+            if p == n_stage1:
+                turn_hb()
             for i in BRANCH_ORDER:
                 if 1 <= p - last_pass[i] <= EPILOGUE_STEPS:
                     epilogue_step(i, p - last_pass[i])
-            if n_stage1 <= p - MULTIPLY_LAG < n_passes:
-                multiply_block(p - MULTIPLY_LAG)
-            if block_that_ends_at(p - BIAS_LAG) is not None:
-                add_bias(block_that_ends_at(p - BIAS_LAG))
-            if block_that_ends_at(p - SQUARE_LAG) is not None:
-                mean_of_squares(block_that_ends_at(p - SQUARE_LAG))
+            for j in range(last_block):
+                step = p - first_turn[j]
+                if 0 <= step < BLOCK_TURNS and p < n_passes - 1 + (j < last_block - 1):
+                    block_step(j, step)
+            if p == n_passes - 3:
+                last_bank = [banks.tile([P, ROWS], F32, name="last_bank", tag="bank") for t in range(N_TILES)]
+                for t in range(N_TILES):
+                    y_acc[last_block, t] = last_bank[t][:]
+            for c in range(BLOCK_PASSES):
+                if p == max(n_passes - 3, n_passes - BLOCK_PASSES + c):
+                    for t in range(N_TILES):
+                        multiply_y(y_acc[last_block, t], last_block, c, t)
+            group(p + GROUP_AHEAD)
 
+        order = [(m, j) for m in range(M_TILES) for j in range(BLOCKS)]
+        for t in range(N_TILES):
+            add_bias(last_block, t, "scalar" if t % 2 == 0 else "vector")
+        for m in range(M_TILES):
+            for j, t in [(last_block - 1, 2), (last_block - 1, 3)] + [(last_block, t) for t in range(N_TILES)]:
+                add_to_gram(j, t, m)
+        for m, j in order[:TURNED_AHEAD]:
+            turn_out(m, j)
         for m in range(M_TILES):
             mean_sq["y", m] = small.tile([P, 1], F32, name="mean_sq_y")
-            nc.vector.reduce_sum(out=mean_sq["y", m][:], in_=block_mean_sq[m][:], axis=mybir.AxisListType.X)
+            diagonal = work.tile([P, P], F32, name="diagonal")
+            nc.vector.scalar_tensor_tensor(
+                out=diagonal[:],
+                in0=gram[m][:],
+                scalar=DETER * EPS,
+                in1=ident_mean[:],
+                op0=ALU.add,
+                op1=ALU.mult,
+                accum_out=mean_sq["y", m][:],
+            )
             rstd["y", m] = power_minus_half(mean_sq["y", m][:])
-        for m in range(M_TILES):
-            for j in range(BLOCKS):
-                cols = slice(j * HID, (j + 1) * HID)
-                nc.vector.scalar_tensor_tensor(
-                    out=y_sb[m][:, cols],
-                    in0=y_sb[m][:, cols],
-                    scalar=rstd["y", m][:],
-                    in1=hg_all[:, cols],
-                    op0=ALU.mult,
-                    op1=ALU.mult,
-                )
-                nc.scalar.activation(out=y_sb[m][:, cols], in_=y_sb[m][:, cols], func=FUNC.Silu)
-                nc.sync.dma_start(out=out[m * P : (m + 1) * P, cols], in_=y_sb[m][:, cols])
+        for k in range(len(order)):
+            m, j = order[k]
+            if k + TURNED_AHEAD < len(order):
+                turn_out(*order[k + TURNED_AHEAD])
+            cols = slice(j * HID, (j + 1) * HID)
+            result = outs.tile([P, HID], F32, name="result")
+            nc.vector.scalar_tensor_tensor(
+                out=result[:],
+                in0=turned_out[m, j][:].rearrange("b t n -> b (t n)"),
+                scalar=rstd["y", m][:],
+                in1=hg_all[:, cols],
+                op0=ALU.mult,
+                op1=ALU.mult,
+            )
+            nc.scalar.activation(out=result[:], in_=result[:], func=FUNC.Silu)
+            nc.sync.dma_start(out=out[m * P : (m + 1) * P, cols], in_=result[:])

@@ -28,7 +28,7 @@ LOAD_AHEAD = 8
 GROUP_AHEAD = 2
 N_TILES = HID // P
 BLOCK_TURNS = 4
-TURNED_AHEAD = 4
+TURNED_AHEAD = 6
 EPILOGUE_STEPS = 7
 RUN = 4
 STAGE1_VECTOR_COLS = 352
@@ -68,7 +68,6 @@ def tile_deter_pa_kernel(
         packed_pool = stack.enter_context(tc.tile_pool(name="packed", bufs=16))
         work = stack.enter_context(tc.tile_pool(name="work", bufs=4))
         small = stack.enter_context(tc.tile_pool(name="small", bufs=6))
-        outs = stack.enter_context(tc.tile_pool(name="outs", bufs=8))
         banks = stack.enter_context(tc.psum_pool(name="banks", bufs=8))
         stack.enter_context(tc.manual_schedule())
 
@@ -213,15 +212,11 @@ def tile_deter_pa_kernel(
                     )
                 if step == 5:
                     if m == 0:
-                        x_turned[i] = banks.tile([P, PACK, M_TILES, P], BF16, name="x_turned", tag="bank")
-                    x_sorted = work.tile([P, PACK, P], BF16, name="x_sorted")
-                    nc.scalar.activation(
-                        out=x_sorted[:].rearrange("b t q -> b q t"),
-                        in_=u_sb[i, m][:].rearrange("b (q t) -> b q t", t=PACK),
-                        func=FUNC.Silu,
-                    )
-                    for t in range(PACK):
-                        nc.tensor.transpose(x_turned[i][:, t, m, :], x_sorted[:, t, :], ident_bf16[:])
+                        x_turned[i] = banks.tile([P, 2, M_TILES, P], F32, name="x_turned", tag="bank")
+                    x_tile = work.tile([P, HID], BF16, name="x_tile")
+                    nc.scalar.activation(out=x_tile[:], in_=u_sb[i, m][:], func=FUNC.Silu)
+                    for k in range(2):
+                        nc.tensor.transpose(x_turned[i][:, k, m, :], x_tile[:].bitcast(F32)[:, k::2], ident_f32[:])
             if step == 2:
                 nc.scalar.activation(out=mean_sq[i][:], in_=mean_sq[i][:], func=FUNC.Copy, bias=EPS)
                 rstd[i] = power_minus_half(mean_sq[i][:])
@@ -229,7 +224,9 @@ def tile_deter_pa_kernel(
                 grouped_rows["x", i] = grouped_pool.tile(
                     [P, ROWS, PACK], BF16, name="grouped_rows", align_bytes=64
                 )
-                nc.scalar.copy(out=grouped_rows["x", i][:], in_=x_turned[i][:].rearrange("q t m b -> q (m b) t"))
+                nc.scalar.copy(
+                    out=grouped_rows["x", i][:].bitcast(F32), in_=x_turned[i][:].rearrange("q u m b -> q (m b) u")
+                )
             if step == 7:
                 quantise_rows(grouped_rows["x", i], x_codes[:, i, :], x_scales[:, i, :])
 
@@ -341,6 +338,8 @@ def tile_deter_pa_kernel(
 
         x_ready = last_pass[0] + EPILOGUE_STEPS
         last_block = BLOCKS - 1
+        order = [(m, j) for m in range(M_TILES) for j in range(BLOCKS)]
+        rstd_at = {2: 0, 6: 1}
         first_turn = [max(n_stage1 + (j + 1) * BLOCK_PASSES, x_ready + 1 + 2 * j) for j in range(last_block)]
         def group(p):
             if p < n_passes:
@@ -377,6 +376,8 @@ def tile_deter_pa_kernel(
                 step = p - first_turn[j]
                 if 0 <= step < BLOCK_TURNS and p < n_passes - 1 + (j < last_block - 1):
                     block_step(j, step)
+            if p >= n_passes - 2:
+                turn_out(*order[p - n_passes + 2])
             if p == n_passes - 3:
                 last_bank = [banks.tile([P, ROWS], F32, name="last_bank", tag="bank") for t in range(N_TILES)]
                 for t in range(N_TILES):
@@ -387,15 +388,7 @@ def tile_deter_pa_kernel(
                         multiply_y(y_acc[last_block, t], last_block, c, t)
             group(p + GROUP_AHEAD)
 
-        order = [(m, j) for m in range(M_TILES) for j in range(BLOCKS)]
-        for t in range(N_TILES):
-            add_bias(last_block, t, "scalar" if t % 2 == 0 else "vector")
-        for m in range(M_TILES):
-            for j, t in [(last_block - 1, 2), (last_block - 1, 3)] + [(last_block, t) for t in range(N_TILES)]:
-                add_to_gram(j, t, m)
-        for m, j in order[:TURNED_AHEAD]:
-            turn_out(m, j)
-        for m in range(M_TILES):
+        def find_rstd(m):
             mean_sq["y", m] = small.tile([P, 1], F32, name="mean_sq_y")
             diagonal = work.tile([P, P], F32, name="diagonal")
             nc.vector.scalar_tensor_tensor(
@@ -408,19 +401,38 @@ def tile_deter_pa_kernel(
                 accum_out=mean_sq["y", m][:],
             )
             rstd["y", m] = power_minus_half(mean_sq["y", m][:])
+
+        result = {}
+        pairs = {}
+
+        def multiply_gain(k):
+            m, j = order[k]
+            if k % 2 == 0:
+                pairs[k // 2] = raw_pool.tile([P, 2, HID], F32, name="pair", tag="raw")
+            result[k] = pairs[k // 2][:, k % 2, :]
+            nc.vector.tensor_tensor(
+                out=result[k],
+                in0=turned_out[m, j][:].rearrange("b t n -> b (t n)"),
+                in1=hg_all[:, j * HID : (j + 1) * HID],
+                op=ALU.mult,
+            )
+
+        multiply_gain(0)
+        for t in range(N_TILES):
+            add_bias(last_block, t, "scalar" if t % 2 == 0 else "vector")
+        for m in range(M_TILES):
+            for j, t in [(last_block - 1, 2), (last_block - 1, 3)] + [(last_block, t) for t in range(N_TILES)]:
+                add_to_gram(j, t, m)
+            if m == 0:
+                for k in range(2, TURNED_AHEAD):
+                    turn_out(*order[k])
+        for k in range(1, len(order)):
+            if k in rstd_at:
+                find_rstd(rstd_at[k])
+            if k - 1 + TURNED_AHEAD < len(order):
+                turn_out(*order[k - 1 + TURNED_AHEAD])
+            multiply_gain(k)
         for k in range(len(order)):
             m, j = order[k]
-            if k + TURNED_AHEAD < len(order):
-                turn_out(*order[k + TURNED_AHEAD])
-            cols = slice(j * HID, (j + 1) * HID)
-            result = outs.tile([P, HID], F32, name="result")
-            nc.vector.scalar_tensor_tensor(
-                out=result[:],
-                in0=turned_out[m, j][:].rearrange("b t n -> b (t n)"),
-                scalar=rstd["y", m][:],
-                in1=hg_all[:, cols],
-                op0=ALU.mult,
-                op1=ALU.mult,
-            )
-            nc.scalar.activation(out=result[:], in_=result[:], func=FUNC.Silu)
-            nc.sync.dma_start(out=out[m * P : (m + 1) * P, cols], in_=result[:])
+            nc.scalar.activation(out=result[k], in_=result[k], func=FUNC.Silu, scale=rstd["y", m][:])
+            nc.sync.dma_start(out=out[m * P : (m + 1) * P, j * HID : (j + 1) * HID], in_=result[k])

@@ -27,8 +27,9 @@ LOAD_PASSES = 2
 LOAD_AHEAD = 8
 GROUP_AHEAD = 2
 N_TILES = HID // P
-BLOCK_TURNS = 4
-TURNED_AHEAD = 6
+EMPTY_LAG = 2
+BLOCK_TURNS = EMPTY_LAG + 3
+GRAM_BLOCKS = BLOCKS - 2
 EPILOGUE_STEPS = 7
 RUN = 4
 STAGE1_VECTOR_COLS = 352
@@ -273,19 +274,26 @@ def tile_deter_pa_kernel(
                 gram.extend(banks.tile([P, P], F32, name="gram%d" % k, tag="bank") for k in range(M_TILES))
             y_tile = y_sb[:, j * N_TILES + t, m * P : (m + 1) * P]
             nc.tensor.matmul(
-                gram[m][:], lhsT=y_tile, rhs=y_tile, start=j == 0 and t == 0, stop=j == BLOCKS - 1 and t == N_TILES - 1
+                gram[m][:], lhsT=y_tile, rhs=y_tile, start=j == 0 and t == 0, stop=j == GRAM_BLOCKS - 1 and t == N_TILES - 1
             )
 
+        def empty_lag(j):
+            return EMPTY_LAG if j < GRAM_BLOCKS else 1
+
+        def empty_step(j, step):
+            for h in range(2):
+                if step == h + empty_lag(j):
+                    for s in range(2):
+                        add_bias(j, 2 * h + s, "scalar")
+
         def block_step(j, step):
-            if step < 2:
-                multiply_half(j, step)
-            if 1 <= step < 3:
-                for s in range(2):
-                    add_bias(j, 2 * (step - 1) + s, "scalar")
-            if step >= 2:
-                for s in range(2):
-                    for m in range(M_TILES):
-                        add_to_gram(j, 2 * (step - 2) + s, m)
+            for h in range(2):
+                if step == h:
+                    multiply_half(j, h)
+                if step == h + empty_lag(j) + 1 and j < GRAM_BLOCKS:
+                    for s in range(2):
+                        for m in range(M_TILES):
+                            add_to_gram(j, 2 * h + s, m)
 
         def turn_out(m, j):
             turned_out[m, j] = banks.tile([P, N_TILES, P], F32, name="turned_out", tag="bank")
@@ -338,8 +346,6 @@ def tile_deter_pa_kernel(
 
         x_ready = last_pass[0] + EPILOGUE_STEPS
         last_block = BLOCKS - 1
-        order = [(m, j) for m in range(M_TILES) for j in range(BLOCKS)]
-        rstd_at = {2: 0, 6: 1}
         first_turn = [max(n_stage1 + (j + 1) * BLOCK_PASSES, x_ready + 1 + 2 * j) for j in range(last_block)]
         def group(p):
             if p < n_passes:
@@ -374,10 +380,10 @@ def tile_deter_pa_kernel(
                     epilogue_step(i, p - last_pass[i])
             for j in range(last_block):
                 step = p - first_turn[j]
-                if 0 <= step < BLOCK_TURNS and p < n_passes - 1 + (j < last_block - 1):
+                if 0 <= step < BLOCK_TURNS:
                     block_step(j, step)
-            if p >= n_passes - 2:
-                turn_out(*order[p - n_passes + 2])
+                    if j < GRAM_BLOCKS:
+                        empty_step(j, step)
             if p == n_passes - 3:
                 last_bank = [banks.tile([P, ROWS], F32, name="last_bank", tag="bank") for t in range(N_TILES)]
                 for t in range(N_TILES):
@@ -387,9 +393,10 @@ def tile_deter_pa_kernel(
                     for t in range(N_TILES):
                         multiply_y(y_acc[last_block, t], last_block, c, t)
             group(p + GROUP_AHEAD)
+            empty_step(last_block - 1, p - first_turn[last_block - 1])
 
-        def find_rstd(m):
-            mean_sq["y", m] = small.tile([P, 1], F32, name="mean_sq_y")
+        def gram_diagonal(m):
+            mean_parts[m] = small.tile([P, 1 + BLOCKS - GRAM_BLOCKS], F32, name="mean_parts")
             diagonal = work.tile([P, P], F32, name="diagonal")
             nc.vector.scalar_tensor_tensor(
                 out=diagonal[:],
@@ -398,41 +405,58 @@ def tile_deter_pa_kernel(
                 in1=ident_mean[:],
                 op0=ALU.add,
                 op1=ALU.mult,
-                accum_out=mean_sq["y", m][:],
+                accum_out=mean_parts[m][:, :1],
             )
+
+        def square(m, j):
+            k = 1 + j - GRAM_BLOCKS
+            squares = work.tile([P, HID], BF16, name="squares")
+            nc.scalar.activation(
+                out=squares[:],
+                in_=turned_out[m, j][:].rearrange("b t n -> b (t n)"),
+                func=FUNC.Square,
+                scale=1.0 / math.sqrt(DETER),
+                accum_out=mean_parts[m][:, k : k + 1],
+            )
+
+        def find_rstd(m):
+            mean_sq["y", m] = small.tile([P, 1], F32, name="mean_sq_y")
+            nc.vector.reduce_sum(out=mean_sq["y", m][:], in_=mean_parts[m][:], axis=mybir.AxisListType.X)
             rstd["y", m] = power_minus_half(mean_sq["y", m][:])
 
-        result = {}
-        pairs = {}
-
-        def multiply_gain(k):
-            m, j = order[k]
+        def multiply_gain(m, j):
+            k = len(result)
             if k % 2 == 0:
                 pairs[k // 2] = raw_pool.tile([P, 2, HID], F32, name="pair", tag="raw")
-            result[k] = pairs[k // 2][:, k % 2, :]
+            result[m, j] = pairs[k // 2][:, k % 2, :]
             nc.vector.tensor_tensor(
-                out=result[k],
+                out=result[m, j],
                 in0=turned_out[m, j][:].rearrange("b t n -> b (t n)"),
                 in1=hg_all[:, j * HID : (j + 1) * HID],
                 op=ALU.mult,
             )
 
-        multiply_gain(0)
+        mean_parts = {}
+        result = {}
+        pairs = {}
+        for m in range(M_TILES):
+            gram_diagonal(m)
+        for m in range(M_TILES):
+            turn_out(m, last_block - 1)
         for t in range(N_TILES):
             add_bias(last_block, t, "scalar" if t % 2 == 0 else "vector")
         for m in range(M_TILES):
-            for j, t in [(last_block - 1, 2), (last_block - 1, 3)] + [(last_block, t) for t in range(N_TILES)]:
-                add_to_gram(j, t, m)
-            if m == 0:
-                for k in range(2, TURNED_AHEAD):
-                    turn_out(*order[k])
-        for k in range(1, len(order)):
-            if k in rstd_at:
-                find_rstd(rstd_at[k])
-            if k - 1 + TURNED_AHEAD < len(order):
-                turn_out(*order[k - 1 + TURNED_AHEAD])
-            multiply_gain(k)
-        for k in range(len(order)):
-            m, j = order[k]
-            nc.scalar.activation(out=result[k], in_=result[k], func=FUNC.Silu, scale=rstd["y", m][:])
-            nc.sync.dma_start(out=out[m * P : (m + 1) * P, j * HID : (j + 1) * HID], in_=result[k])
+            turn_out(m, last_block)
+            square(m, last_block - 1)
+            multiply_gain(m, last_block - 1)
+            square(m, last_block)
+            find_rstd(m)
+            multiply_gain(m, last_block)
+        for m in range(M_TILES):
+            for j in range(last_block - 1):
+                turn_out(m, j)
+                multiply_gain(m, j)
+        for m in range(M_TILES):
+            for j in (last_block - 1, last_block) + tuple(range(last_block - 1)):
+                nc.scalar.activation(out=result[m, j], in_=result[m, j], func=FUNC.Silu, scale=rstd["y", m][:])
+                nc.sync.dma_start(out=out[m * P : (m + 1) * P, j * HID : (j + 1) * HID], in_=result[m, j])

@@ -28,12 +28,12 @@ LOAD_AHEAD = 8
 GROUP_AHEAD = 2
 N_TILES = HID // P
 EMPTY_LAG = 2
-BLOCK_TURNS = EMPTY_LAG + 3
+BLOCK_TURNS = EMPTY_LAG + 5
 GRAM_BLOCKS = BLOCKS - 2
 EPILOGUE_STEPS = 7
 RUN = 4
 STAGE1_VECTOR_COLS = 352
-STAGE2_VECTOR_COLS = 288
+STAGE2_VECTOR_COLS = 304
 
 FLOPS = 2 * BATCH * (DETER + 1024 + 512) * HID + 2 * BATCH * BLOCK_PASSES * K_PASS * DETER
 
@@ -84,6 +84,10 @@ def tile_deter_pa_kernel(
         hb_columns = keep.tile([P, BLOCKS * N_TILES], F32)
         hg_all = keep.tile([P, DETER], BF16)
         y_sb = keep.tile([P, BLOCKS * N_TILES, ROWS], F32)
+        squared_blocks = (0,)
+        gram_blocks = [j for j in range(GRAM_BLOCKS) if j not in squared_blocks]
+        all_squared = squared_blocks + (BLOCKS - 2, BLOCKS - 1)
+        mean_parts = [keep.tile([P, 1 + len(all_squared)], F32, name="mean_parts%d" % m) for m in range(M_TILES)]
         gram = []
         y_acc = {}
         turned_out = {}
@@ -270,11 +274,22 @@ def tile_deter_pa_kernel(
                 )
 
         def add_to_gram(j, t, m):
-            if j == 0 and t == 0 and m == 0:
+            if j == gram_blocks[0] and t == 0 and m == 0:
                 gram.extend(banks.tile([P, P], F32, name="gram%d" % k, tag="bank") for k in range(M_TILES))
             y_tile = y_sb[:, j * N_TILES + t, m * P : (m + 1) * P]
             nc.tensor.matmul(
-                gram[m][:], lhsT=y_tile, rhs=y_tile, start=j == 0 and t == 0, stop=j == GRAM_BLOCKS - 1 and t == N_TILES - 1
+                gram[m][:], lhsT=y_tile, rhs=y_tile, start=j == gram_blocks[0] and t == 0, stop=j == gram_blocks[-1] and t == N_TILES - 1
+            )
+
+        def square(m, j):
+            k = 1 + all_squared.index(j)
+            squares = work.tile([P, HID], BF16, name="squares")
+            nc.scalar.activation(
+                out=squares[:],
+                in_=turned_out[m, j][:].rearrange("b t n -> b (t n)"),
+                func=FUNC.Square,
+                scale=1.0 / math.sqrt(DETER),
+                accum_out=mean_parts[m][:, k : k + 1],
             )
 
         def empty_lag(j):
@@ -290,10 +305,15 @@ def tile_deter_pa_kernel(
             for h in range(2):
                 if step == h:
                     multiply_half(j, h)
-                if step == h + empty_lag(j) + 1 and j < GRAM_BLOCKS:
+                if step == h + empty_lag(j) + 1 and j in gram_blocks:
                     for s in range(2):
                         for m in range(M_TILES):
                             add_to_gram(j, 2 * h + s, m)
+            if j in squared_blocks and step == EMPTY_LAG + 2:
+                for m in range(M_TILES):
+                    turn_out(m, j)
+            if j in squared_blocks and EMPTY_LAG + 3 <= step:
+                square(step - EMPTY_LAG - 3, j)
 
         def turn_out(m, j):
             turned_out[m, j] = banks.tile([P, N_TILES, P], F32, name="turned_out", tag="bank")
@@ -396,7 +416,6 @@ def tile_deter_pa_kernel(
             empty_step(last_block - 1, p - first_turn[last_block - 1])
 
         def gram_diagonal(m):
-            mean_parts[m] = small.tile([P, 1 + BLOCKS - GRAM_BLOCKS], F32, name="mean_parts")
             diagonal = work.tile([P, P], F32, name="diagonal")
             nc.vector.scalar_tensor_tensor(
                 out=diagonal[:],
@@ -406,17 +425,6 @@ def tile_deter_pa_kernel(
                 op0=ALU.add,
                 op1=ALU.mult,
                 accum_out=mean_parts[m][:, :1],
-            )
-
-        def square(m, j):
-            k = 1 + j - GRAM_BLOCKS
-            squares = work.tile([P, HID], BF16, name="squares")
-            nc.scalar.activation(
-                out=squares[:],
-                in_=turned_out[m, j][:].rearrange("b t n -> b (t n)"),
-                func=FUNC.Square,
-                scale=1.0 / math.sqrt(DETER),
-                accum_out=mean_parts[m][:, k : k + 1],
             )
 
         def find_rstd(m):
@@ -436,7 +444,6 @@ def tile_deter_pa_kernel(
                 op=ALU.mult,
             )
 
-        mean_parts = {}
         result = {}
         pairs = {}
         for m in range(M_TILES):

import math
from contextlib import ExitStack

import concourse.mybir as mybir
from concourse.masks import make_identity

BF16 = mybir.dt.bfloat16
F32 = mybir.dt.float32
I32 = mybir.dt.int32
U32 = mybir.dt.uint32
U8 = mybir.dt.uint8
FP8X4 = mybir.dt.float8_e4m3fn_x4
ALU = mybir.AluOpType
FUNC = mybir.ActivationFunctionType

P = 128
PACK = 4
K_PASS = P * PACK
BATCH, DETER, HID, BLOCKS = 256, 4096, 512, 8
M_TILES = BATCH // P
ROWS = M_TILES * P
BRANCHES = 3
BRANCH_ORDER = (2, 1, 0)
BLOCK_PASSES = 1 + BRANCHES
EPS = 1e-4
LOAD_PASSES = 2
LOAD_AHEAD = 8
GROUP_AHEAD = 2
N_TILES = HID // P
EMPTY_LAG = 2
BLOCK_TURNS = EMPTY_LAG + 5
GRAM_BLOCKS = BLOCKS - 2
EPILOGUE_STEPS = 7
RUN = 4
STAGE1_VECTOR_COLS = 352
STAGE2_VECTOR_COLS = 304

FLOPS = 2 * BATCH * (DETER + 1024 + 512) * HID + 2 * BATCH * BLOCK_PASSES * K_PASS * DETER


def tile_deter_pa_kernel(
    tc, deter, stoch, action, w0, b0, g0, w1, b1, g1, w2, b2, g2, hw0, hb0, hg0, out
):
    nc = tc.nc
    inputs = (deter, stoch, action)
    weights = (w0, w1, w2)

    weight_rows = []
    stage1 = []
    last_pass = {}
    for i in BRANCH_ORDER:
        for g in range(inputs[i].shape[1] // K_PASS):
            weight_rows.append(weights[i][g * K_PASS : (g + 1) * K_PASS, :])
            stage1.append((i, g))
        last_pass[i] = len(stage1) - 1
    block_parts = (0,) + tuple(1 + i for i in BRANCH_ORDER)
    for j in range(BLOCKS):
        for part in block_parts:
            weight_rows.append(hw0[j, part * K_PASS : (part + 1) * K_PASS, :])
    n_stage1 = len(stage1)
    n_passes = len(weight_rows)

    with ExitStack() as stack:
        const = stack.enter_context(tc.tile_pool(name="const", bufs=1))
        keep = stack.enter_context(tc.tile_pool(name="keep", bufs=1))
        acts = stack.enter_context(tc.tile_pool(name="acts", bufs=2))
        raw_pool = stack.enter_context(tc.tile_pool(name="raw", bufs=8))
        grouped_pool = stack.enter_context(tc.tile_pool(name="grouped", bufs=5))
        packed_pool = stack.enter_context(tc.tile_pool(name="packed", bufs=16))
        work = stack.enter_context(tc.tile_pool(name="work", bufs=4))
        small = stack.enter_context(tc.tile_pool(name="small", bufs=6))
        banks = stack.enter_context(tc.psum_pool(name="banks", bufs=8))
        stack.enter_context(tc.manual_schedule())

        in_codes = {}
        in_scales = {}
        for i in range(BRANCHES):
            n = inputs[i].shape[1] // K_PASS
            in_codes[i] = keep.tile([P, n, ROWS], U32, name="in_codes%d" % i, align_bytes=64)
            in_scales[i] = keep.tile([P, n, ROWS], U8, name="in_scales%d" % i, align_bytes=64)
        x_codes = keep.tile([P, BRANCHES, ROWS], U32, align_bytes=64)
        x_scales = keep.tile([P, BRANCHES, ROWS], U8, align_bytes=64)
        branch_vectors = keep.tile([P, 2 * BRANCHES, HID], BF16)
        hb_columns = keep.tile([P, BLOCKS * N_TILES], F32)
        hg_all = keep.tile([P, DETER], BF16)
        y_sb = keep.tile([P, BLOCKS * N_TILES, ROWS], F32)
        squared_blocks = (0,)
        gram_blocks = [j for j in range(GRAM_BLOCKS) if j not in squared_blocks]
        all_squared = squared_blocks + (BLOCKS - 2, BLOCKS - 1)
        mean_parts = [keep.tile([P, 1 + len(all_squared)], F32, name="mean_parts%d" % m) for m in range(M_TILES)]
        gram = []
        y_acc = {}
        turned_out = {}

        raw = {}
        grouped = {}
        packed = {}
        x_sb = {}
        turned = {}
        grouped_rows = {}
        acc = {}
        u_sb = {}
        rstd = {}
        mean_sq = {}
        x_turned = {}

        def load(p):
            raw[p] = raw_pool.tile([P, PACK, HID], BF16, name="raw")
            nc.sync.dma_start(out=raw[p][:], in_=weight_rows[p].rearrange("(q t) n -> q t n", t=PACK))
            if p < n_stage1 and stage1[p][1] % LOAD_PASSES == 0:
                i, g = stage1[p]
                n = min(LOAD_PASSES * K_PASS, inputs[i].shape[1] - g * K_PASS)
                x_sb[p] = acts.tile([P, M_TILES, n], BF16, name="x_sb%d" % i)
                for m in range(M_TILES):
                    nc.sync.dma_start(
                        out=x_sb[p][:, m, :], in_=inputs[i][m * P : (m + 1) * P, g * K_PASS : g * K_PASS + n]
                    )
            if p == LOAD_AHEAD:
                nc.sync.dma_start(out=hb_rows[: BLOCKS * N_TILES, :], in_=hb0.rearrange("(c n) -> c n", n=P))
            if p == n_passes - 1:
                nc.sync.dma_start(out=hg_all[:], in_=hg0.partition_broadcast(P))

        def regroup(p):
            grouped[p] = grouped_pool.tile([P, HID, PACK], BF16, name="grouped", align_bytes=64)
            src = raw[p][:].rearrange("q t (c i) -> q c t i", i=RUN)
            dst = grouped[p][:].rearrange("q (c i) t -> q c t i", i=RUN)
            split = (STAGE1_VECTOR_COLS if p < n_stage1 else STAGE2_VECTOR_COLS) // RUN
            nc.vector.tensor_copy(out=dst[:, :split], in_=src[:, :split])
            nc.scalar.copy(out=dst[:, split:], in_=src[:, split:])

        def quantise(p):
            codes = packed_pool.tile([P, HID], U32, name="codes", align_bytes=64)
            scales = packed_pool.tile([P, HID], U8, name="scales", align_bytes=64)
            nc.vector.quantize_mx(
                out=codes[:].bitcast(FP8X4), scales=scales[:], in_=grouped[p][:].rearrange("q n t -> q (n t)")
            )
            packed[p] = (codes, scales)

        def turn(p):
            g = stage1[p][1]
            words = x_sb[p - g % LOAD_PASSES][:].bitcast(F32)
            first = (g % LOAD_PASSES) * (K_PASS // 2)
            turned[p] = banks.tile([P, 2, M_TILES, P], F32, name="turned", tag="bank")
            for m in range(M_TILES):
                for u in range(2):
                    nc.tensor.transpose(
                        turned[p][:, u, m, :], words[:, m, first + u : first + K_PASS // 2 : 2], ident_f32[:]
                    )

        def empty(p):
            grouped_rows[p] = grouped_pool.tile([P, ROWS, PACK], BF16, name="grouped_rows", align_bytes=64)
            if stage1[p][0] == 2:
                nc.vector.tensor_scalar(
                    out=grouped_rows[p][:].rearrange("q r (u e) -> q r u e", e=2),
                    in0=turned[p][:].bitcast(BF16).rearrange("q u m (b e) -> q (m b) u e", e=2),
                    scalar1=-1.0,
                    scalar2=1.0,
                    op0=ALU.max,
                    op1=ALU.min,
                )
            else:
                nc.scalar.copy(
                    out=grouped_rows[p][:].bitcast(F32), in_=turned[p][:].rearrange("q u m b -> q (m b) u")
                )

        def quantise_rows(tile, codes, scales):
            nc.vector.quantize_mx(
                out=codes.bitcast(FP8X4), scales=scales, in_=tile[:].rearrange("q r t -> q (r t)")
            )

        def multiply(p, acc_tiles, lhs_codes, lhs_scales, start, stop):
            for m in range(M_TILES):
                nc.tensor.matmul_mx(
                    out=acc_tiles[m][:],
                    lhsT=lhs_codes[:, m * P : (m + 1) * P].bitcast(FP8X4),
                    lhsT_scale=lhs_scales[:, m * P : (m + 1) * P],
                    rhs=packed[p][0][:].bitcast(FP8X4),
                    rhs_scale=packed[p][1][:],
                    start=start,
                    stop=stop,
                )

        def new_acc():
            return [banks.tile([P, HID], F32, name="acc%d" % m, tag="bank") for m in range(M_TILES)]

        def power_minus_half(value):
            result = small.tile(list(value.shape), F32, name="rstd")
            nc.gpsimd.tensor_tensor(out=result[:], in0=value, in1=minus_half[:, : value.shape[1]], op=ALU.pow)
            return result

        def epilogue_step(i, step):
            for m in range(M_TILES):
                if step == 1:
                    u_sb[i, m] = work.tile([P, HID], F32, name="u_sb")
                    nc.vector.tensor_tensor(
                        out=u_sb[i, m][:], in0=acc[i][m][:], in1=branch_vectors[:, 2 * i, :], op=ALU.add
                    )
                if step == 2:
                    if m == 0:
                        mean_sq[i] = small.tile([P, M_TILES], F32, name="mean_sq")
                    squares = work.tile([P, HID], BF16, name="squares")
                    nc.scalar.activation(
                        out=squares[:],
                        in_=u_sb[i, m][:],
                        func=FUNC.Square,
                        scale=1.0 / math.sqrt(HID),
                        accum_out=mean_sq[i][:, m : m + 1],
                    )
                if step == 4:
                    nc.vector.scalar_tensor_tensor(
                        out=u_sb[i, m][:],
                        in0=u_sb[i, m][:],
                        scalar=rstd[i][:, m : m + 1],
                        in1=branch_vectors[:, 2 * i + 1, :],
                        op0=ALU.mult,
                        op1=ALU.mult,
                    )
                if step == 5:
                    if m == 0:
                        x_turned[i] = banks.tile([P, 2, M_TILES, P], F32, name="x_turned", tag="bank")
                    x_tile = work.tile([P, HID], BF16, name="x_tile")
                    nc.scalar.activation(out=x_tile[:], in_=u_sb[i, m][:], func=FUNC.Silu)
                    for k in range(2):
                        nc.tensor.transpose(x_turned[i][:, k, m, :], x_tile[:].bitcast(F32)[:, k::2], ident_f32[:])
            if step == 2:
                nc.scalar.activation(out=mean_sq[i][:], in_=mean_sq[i][:], func=FUNC.Copy, bias=EPS)
                rstd[i] = power_minus_half(mean_sq[i][:])
            if step == 6:
                grouped_rows["x", i] = grouped_pool.tile(
                    [P, ROWS, PACK], BF16, name="grouped_rows", align_bytes=64
                )
                nc.scalar.copy(
                    out=grouped_rows["x", i][:].bitcast(F32), in_=x_turned[i][:].rearrange("q u m b -> q (m b) u")
                )
            if step == 7:
                quantise_rows(grouped_rows["x", i], x_codes[:, i, :], x_scales[:, i, :])

        def block_operands(j, c):
            p = n_stage1 + j * BLOCK_PASSES + c
            if c == 0:
                return packed[p], in_codes[0][:, j, :], in_scales[0][:, j, :]
            i = block_parts[c] - 1
            return packed[p], x_codes[:, i, :], x_scales[:, i, :]

        def multiply_y(out, j, c, t):
            (codes, scales), rhs_codes, rhs_scales = block_operands(j, c)
            cols = slice(t * P, (t + 1) * P)
            nc.tensor.matmul_mx(
                out=out,
                lhsT=codes[:, cols].bitcast(FP8X4),
                lhsT_scale=scales[:, cols],
                rhs=rhs_codes.bitcast(FP8X4),
                rhs_scale=rhs_scales,
                start=c == 0,
                stop=c == BLOCK_PASSES - 1,
            )

        def multiply_half(j, h):
            bank = banks.tile([P, 2, ROWS], F32, name="y_acc", tag="bank")
            for s in range(2):
                for c in range(BLOCK_PASSES):
                    multiply_y(bank[:, s, :], j, c, 2 * h + s)
                y_acc[j, 2 * h + s] = bank[:, s, :]

        def add_bias(j, t, engine):
            n = j * N_TILES + t
            if engine == "scalar":
                nc.scalar.activation(
                    out=y_sb[:, n, :], in_=y_acc[j, t], func=FUNC.Identity, bias=hb_columns[:, n : n + 1]
                )
            else:
                nc.vector.tensor_scalar(
                    out=y_sb[:, n, :], in0=y_acc[j, t], scalar1=hb_columns[:, n : n + 1], scalar2=None, op0=ALU.add
                )

        def add_to_gram(j, t, m):
            if j == gram_blocks[0] and t == 0 and m == 0:
                gram.extend(banks.tile([P, P], F32, name="gram%d" % k, tag="bank") for k in range(M_TILES))
            y_tile = y_sb[:, j * N_TILES + t, m * P : (m + 1) * P]
            nc.tensor.matmul(
                gram[m][:], lhsT=y_tile, rhs=y_tile, start=j == gram_blocks[0] and t == 0, stop=j == gram_blocks[-1] and t == N_TILES - 1
            )

        def square(m, j):
            k = 1 + all_squared.index(j)
            squares = work.tile([P, HID], BF16, name="squares")
            nc.scalar.activation(
                out=squares[:],
                in_=turned_out[m, j][:].rearrange("b t n -> b (t n)"),
                func=FUNC.Square,
                scale=1.0 / math.sqrt(DETER),
                accum_out=mean_parts[m][:, k : k + 1],
            )

        def empty_lag(j):
            return EMPTY_LAG if j < GRAM_BLOCKS else 1

        def empty_step(j, step):
            for h in range(2):
                if step == h + empty_lag(j):
                    for s in range(2):
                        add_bias(j, 2 * h + s, "scalar")

        def block_step(j, step):
            for h in range(2):
                if step == h:
                    multiply_half(j, h)
                if step == h + empty_lag(j) + 1 and j in gram_blocks:
                    for s in range(2):
                        for m in range(M_TILES):
                            add_to_gram(j, 2 * h + s, m)
            if j in squared_blocks and step == EMPTY_LAG + 2:
                for m in range(M_TILES):
                    turn_out(m, j)
            if j in squared_blocks and EMPTY_LAG + 3 <= step:
                square(step - EMPTY_LAG - 3, j)

        def turn_out(m, j):
            turned_out[m, j] = banks.tile([P, N_TILES, P], F32, name="turned_out", tag="bank")
            for t in range(N_TILES):
                nc.tensor.transpose(
                    turned_out[m, j][:, t, :], y_sb[:, j * N_TILES + t, m * P : (m + 1) * P], ident_f32[:]
                )

        warm = const.tile([P, 1], F32)
        nc.vector.memset(warm[:], 0.0)
        nc.scalar.activation(out=warm[:], in_=warm[:], func=FUNC.Silu)
        vector_row = const.tile([P, 2 * BRANCHES, HID], BF16)
        nc.vector.memset(vector_row[:].bitcast(I32), 0)
        branch_rows = ((b0, g0), (b1, g1), (b2, g2))
        for p in range(LOAD_AHEAD):
            load(p)
            if p < BRANCHES:
                i = BRANCH_ORDER[p]
                for h, vec in enumerate(branch_rows[i]):
                    nc.sync.dma_start(out=vector_row[0:1, 2 * i + h, :], in_=vec.rearrange("(o n) -> o n", o=1))
        ones = const.tile([P, P], BF16)
        nc.vector.memset(ones[:], 1.0)
        minus_half = const.tile([P, M_TILES], F32)
        nc.vector.memset(minus_half[:], -0.5)
        hb_rows = const.tile([P, P], BF16)
        nc.vector.memset(hb_rows[:].bitcast(I32), 0)
        ident_f32 = const.tile([P, P], F32)
        make_identity(nc, ident_f32[:])
        ident_bf16 = const.tile([P, P], BF16)
        make_identity(nc, ident_bf16[:])
        ident_mean = const.tile([P, P], F32)
        nc.scalar.mul(ident_mean[:], ident_f32[:], 1.0 / DETER)

        spread = {}

        def spread_vectors(i):
            spread[i] = banks.tile([P, 2, HID], BF16, name="spread", tag="bank")
            for h in range(2):
                nc.tensor.matmul(
                    spread[i][:, h, :], lhsT=ones[:], rhs=vector_row[:, 2 * i + h, :], start=True, stop=True
                )

        def empty_spread(i):
            nc.scalar.copy(out=branch_vectors[:, 2 * i : 2 * i + 2, :], in_=spread[i][:])

        def turn_hb():
            bank = banks.tile([P, P], BF16, name="hb_bank", tag="bank")
            nc.tensor.transpose(bank[:], hb_rows[:], ident_bf16[:])
            nc.scalar.copy(out=hb_columns[:], in_=bank[:, : BLOCKS * N_TILES])

        x_ready = last_pass[0] + EPILOGUE_STEPS
        last_block = BLOCKS - 1
        first_turn = [max(n_stage1 + (j + 1) * BLOCK_PASSES, x_ready + 1 + 2 * j) for j in range(last_block)]
        def group(p):
            if p < n_passes:
                regroup(p)
            if p + 1 < n_stage1:
                turn(p + 1)
            if p < n_stage1:
                empty(p)

        turn(0)
        spread_vectors(BRANCH_ORDER[0])
        for p in range(GROUP_AHEAD):
            group(p)
        for p in range(n_passes):
            if p + LOAD_AHEAD < n_passes:
                load(p + LOAD_AHEAD)
            quantise(p)
            if p < n_stage1:
                i, g = stage1[p]
                quantise_rows(grouped_rows[p], in_codes[i][:, g, :], in_scales[i][:, g, :])
                if g == 0:
                    acc[i] = new_acc()
                multiply(p, acc[i], in_codes[i][:, g, :], in_scales[i][:, g, :], g == 0, p == last_pass[i])
            if p < BRANCHES:
                empty_spread(BRANCH_ORDER[p])
            if p + 1 < BRANCHES:
                spread_vectors(BRANCH_ORDER[p + 1])
            if p == n_stage1:
                turn_hb()
            for i in BRANCH_ORDER:
                if 1 <= p - last_pass[i] <= EPILOGUE_STEPS:
                    epilogue_step(i, p - last_pass[i])
            for j in range(last_block):
                step = p - first_turn[j]
                if 0 <= step < BLOCK_TURNS:
                    block_step(j, step)
                    if j < GRAM_BLOCKS:
                        empty_step(j, step)
            if p == n_passes - 3:
                last_bank = [banks.tile([P, ROWS], F32, name="last_bank", tag="bank") for t in range(N_TILES)]
                for t in range(N_TILES):
                    y_acc[last_block, t] = last_bank[t][:]
            for c in range(BLOCK_PASSES):
                if p == max(n_passes - 3, n_passes - BLOCK_PASSES + c):
                    for t in range(N_TILES):
                        multiply_y(y_acc[last_block, t], last_block, c, t)
            group(p + GROUP_AHEAD)
            empty_step(last_block - 1, p - first_turn[last_block - 1])

        def gram_diagonal(m):
            diagonal = work.tile([P, P], F32, name="diagonal")
            nc.vector.scalar_tensor_tensor(
                out=diagonal[:],
                in0=gram[m][:],
                scalar=DETER * EPS,
                in1=ident_mean[:],
                op0=ALU.add,
                op1=ALU.mult,
                accum_out=mean_parts[m][:, :1],
            )

        def find_rstd(m):
            mean_sq["y", m] = small.tile([P, 1], F32, name="mean_sq_y")
            nc.vector.reduce_sum(out=mean_sq["y", m][:], in_=mean_parts[m][:], axis=mybir.AxisListType.X)
            rstd["y", m] = power_minus_half(mean_sq["y", m][:])

        def multiply_gain(m, j):
            k = len(result)
            if k % 2 == 0:
                pairs[k // 2] = raw_pool.tile([P, 2, HID], F32, name="pair", tag="raw")
            result[m, j] = pairs[k // 2][:, k % 2, :]
            nc.vector.tensor_tensor(
                out=result[m, j],
                in0=turned_out[m, j][:].rearrange("b t n -> b (t n)"),
                in1=hg_all[:, j * HID : (j + 1) * HID],
                op=ALU.mult,
            )

        result = {}
        pairs = {}
        for m in range(M_TILES):
            gram_diagonal(m)
        for m in range(M_TILES):
            turn_out(m, last_block - 1)
        for t in range(N_TILES):
            add_bias(last_block, t, "scalar" if t % 2 == 0 else "vector")
        for m in range(M_TILES):
            turn_out(m, last_block)
            square(m, last_block - 1)
            multiply_gain(m, last_block - 1)
            square(m, last_block)
            find_rstd(m)
            multiply_gain(m, last_block)
        for m in range(M_TILES):
            for j in range(last_block - 1):
                turn_out(m, j)
                multiply_gain(m, j)
        for m in range(M_TILES):
            for j in (last_block - 1, last_block) + tuple(range(last_block - 1)):
                nc.scalar.activation(out=result[m, j], in_=result[m, j], func=FUNC.Silu, scale=rstd["y", m][:])
                nc.sync.dma_start(out=out[m * P : (m + 1) * P, j * HID : (j + 1) * HID], in_=result[m, j])
